import numpy as np
import ml_dtypes


def mxq(x, axis, fmt="e4m3"):
    dtype, down = {"e4m3": (ml_dtypes.float8_e4m3fn, 7), "e5m2": (ml_dtypes.float8_e5m2, 14)}[fmt]
    v = np.moveaxis(np.asarray(x, np.float32).astype(ml_dtypes.bfloat16).astype(np.float64), axis, -1)
    blocks = v.reshape(v.shape[:-1] + (-1, 32))
    amax = np.abs(blocks).max(-1, keepdims=True)
    byte = np.maximum(np.where(amax > 0, np.frexp(amax)[1] - 1 + 127, 0) - down, 1)
    scale = np.exp2(byte - 127.0)
    codes = (blocks / scale).astype(np.float32).astype(dtype).astype(np.float64)
    return np.moveaxis((codes * scale).reshape(v.shape), -1, axis)


WIDE = False


def mx_kscale(k):
    if not WIDE:
        return np.ones(k)
    levels = np.array([10, -10, 5, -5, 0])
    if k % 512:
        return np.exp2(np.random.permutation(np.resize(levels, k // 32))).repeat(32)
    a = np.empty((k // 512, 16))
    for p in range(k // 512):
        a[p, :8] = np.random.permutation(np.resize(levels, 8))
        for g in range(8):
            far = levels[np.abs(levels - a[p, g]) >= 10]
            a[p, g + 8] = far[np.random.randint(len(far))]
    return np.exp2(a.ravel()).repeat(32)


BF16 = ml_dtypes.bfloat16


def bf(x):
    return np.asarray(x, np.float32).astype(BF16)


def f64(x):
    return np.asarray(x).astype(np.float64)


N, K, D_IN, HC, H = 256, 8, 1024, 1024, 1024


def sigmoid(v):
    return 1.0 / (1.0 + np.exp(-v))


def setup_inputs():
    s, t = mx_kscale(D_IN), mx_kscale(HC)
    return {
        "x": bf(np.random.standard_normal((N, D_IN)) * s),
        "child_h": bf(np.random.standard_normal((N, K, HC)) * t),
        "child_c": bf(np.random.standard_normal((N, K, H)) * 0.5),
        "Wf": bf(np.random.standard_normal((D_IN, H)) * 0.7 / np.sqrt(D_IN) / s[:, None]),
        "bWf": bf(np.random.standard_normal(H) * 0.3),
        "Uf": bf(np.random.standard_normal((HC, H)) * 0.7 / np.sqrt(HC) / t[:, None]),
        "bUf": bf(np.random.standard_normal(H) * 0.3),
    }


def core(x, child_h, child_c, Wf, bWf, Uf, bUf):
    xf = (mxq(f64(x), 1, "e4m3") @ mxq(f64(Wf), 0, "e4m3")) + f64(bWf)
    hf = mxq(f64(child_h), 2, "e4m3") @ mxq(f64(Uf), 0, "e4m3")
    f = sigmoid(xf[:, None, :] + hf + f64(bUf))
    return (f * f64(child_c)).sum(axis=1)


def e4m3fn_bytes(y):
    return np.clip(np.asarray(y, np.float64), -448.0, 448.0).astype(np.float32).astype(ml_dtypes.float8_e4m3fn).view(np.uint8)


def reference(x, child_h, child_c, Wf, bWf, Uf, bUf):
    out = core(x, child_h, child_c, Wf, bWf, Uf, bUf)
    s = np.max(np.abs(out)) / 448.0
    return out, e4m3fn_bytes(out / s)

@@ -1,0 +1,372 @@
+from contextlib import ExitStack
+
+import concourse.mybir as mybir
+from concourse.masks import make_identity
+
+F32 = mybir.dt.float32
+BF16 = mybir.dt.bfloat16
+U32 = mybir.dt.uint32
+U8 = mybir.dt.uint8
+FP8 = mybir.dt.float8_e4m3fn
+FP8X4 = mybir.dt.float8_e4m3fn_x4
+ACT = mybir.ActivationFunctionType
+ALU = mybir.AluOpType
+AX = mybir.AxisListType
+
+P = 128
+NODES, KIDS, D, H = 256, 8, 1024, 1024
+FLOPS = 2 * (NODES + NODES * KIDS) * D * H
+
+
+def tile_childsumtreelstmcell_pa_kernel(tc, x, child_h, child_c, Wf, bWf, Uf, bUf, out_0, out_1):
+    nc = tc.nc
+    with ExitStack() as ctx:
+        keep = ctx.enter_context(tc.tile_pool(name="keep", bufs=1))
+        wst = ctx.enter_context(tc.tile_pool(name="wst", bufs=4))
+        hst = ctx.enter_context(tc.tile_pool(name="hst", bufs=3))
+        zzp = ctx.enter_context(tc.tile_pool(name="zzp", bufs=3))
+        fpl = ctx.enter_context(tc.tile_pool(name="fpl", bufs=4))
+        ppl = ctx.enter_context(tc.tile_pool(name="ppl", bufs=4))
+        ps_z = ctx.enter_context(tc.psum_pool(name="ps_z", bufs=3))
+        ps_ct = ctx.enter_context(tc.psum_pool(name="ps_ct", bufs=2))
+        ps_tr = ctx.enter_context(tc.psum_pool(name="ps_tr", bufs=2))
+        ps_o = ctx.enter_context(tc.psum_pool(name="ps_o", bufs=1))
+
+        ident_f = keep.tile([P, P], F32, name="ident_f")
+        make_identity(nc, ident_f[:])
+        ident_b = keep.tile([P, P], BF16, name="ident_b")
+        make_identity(nc, ident_b[:])
+        zero_col = keep.tile([P, 1], F32, name="zero_col")
+        nc.vector.memset(zero_col[:], 0.0)
+        warm = keep.tile([P, 1], F32, name="warm")
+        nc.scalar.activation(out=warm[:], in_=zero_col[:], func=ACT.Sigmoid)
+        brow = keep.tile([P, P], BF16, name="brow")
+        nc.vector.memset(brow[:], 0.0)
+        nc.scalar.dma_start(out=brow[0:8, :], in_=bWf.rearrange("(j p) -> j p", p=P))
+        nc.scalar.dma_start(out=brow[8:16, :], in_=bUf.rearrange("(j p) -> j p", p=P))
+
+        def load(name, shape, src):
+            t = keep.tile(shape, BF16, name=name)
+            nc.sync.dma_start(out=t[:], in_=src)
+            return t
+
+        def load_w(m, g, c0, c1):
+            src = (Wf, Uf)[m][512 * g : 512 * (g + 1), c0:c1].rearrange("(p t) w -> p t w", t=4)
+            return load("wraw%d_%d_%d" % (m, g, c0), [P, 4, c1 - c0], src)
+
+        def load_h(a, q):
+            return load("h%d_%d" % (a, q), [P, 4, D], child_h[P * a : P * (a + 1), 4 * q : 4 * q + 4, :])
+
+        def load_c(a, c0, c1):
+            return load("c%d_%d" % (a, c0), [P, KIDS, c1 - c0], child_c[P * a : P * (a + 1), :, c0:c1])
+
+        wraw = {}
+        h_sb = {}
+        c_sb = {}
+        h_sb[(0, 0)] = load_h(0, 0)
+        x_sb = load("x_sb", [P, 2, D], x.rearrange("(a p) d -> p a d", p=P))
+        for m in (0, 1):
+            for g in (0, 1):
+                wraw[(m, g, 0)] = load_w(m, g, 0, 256)
+        h_sb[(0, 1)] = load_h(0, 1)
+        c_sb[(0, 0)] = load_c(0, 0, 256)
+        for m in (0, 1):
+            for g in (0, 1):
+                wraw[(m, g, 1)] = load_w(m, g, 256, 512)
+        c_sb[(0, 1)] = load_c(0, 256, 512)
+        h_sb[(1, 0)] = load_h(1, 0)
+        h_sb[(1, 1)] = load_h(1, 1)
+        c_sb[(1, 0)] = load_c(1, 0, 512)
+        for m in (0, 1):
+            for g in (0, 1):
+                wraw[(m, g, 2)] = load_w(m, g, 512, 1024)
+        c_sb[(0, 2)] = load_c(0, 512, 1024)
+        c_sb[(1, 2)] = load_c(1, 512, 1024)
+
+        def c_block(a, j, k):
+            if j >= 4:
+                return c_sb[(a, 2)][:, k, P * (j - 4) : P * (j - 3)]
+            if a == 1:
+                return c_sb[(1, 0)][:, k, P * j : P * (j + 1)]
+            return c_sb[(0, j // 2)][:, k, P * (j % 2) : P * (j % 2 + 1)]
+
+        w_codes = keep.tile([P, 2, 2, H], U32, name="w_codes", align_bytes=64)
+        w_scales = keep.tile([P, 2, 2, H], U8, name="w_scales", align_bytes=64)
+        h_codes = keep.tile([P, 2, 2, KIDS * P], U32, name="h_codes", align_bytes=64)
+        h_scales = keep.tile([P, 2, 2, KIDS * P], U8, name="h_scales", align_bytes=64)
+        x_codes = keep.tile([P, 2, NODES], U32, name="x_codes", align_bytes=64)
+        x_scales = keep.tile([P, 2, NODES], U8, name="x_scales", align_bytes=64)
+        xfT = keep.tile([P, 8, NODES], F32, name="xfT")
+        out_sb = keep.tile([P, 2, H], F32, name="out_sb")
+        stats = keep.tile([P, 8], F32, name="stats")
+
+        def copy_on(eng, out, in_):
+            if eng == "v":
+                nc.vector.tensor_copy(out=out, in_=in_)
+            else:
+                nc.scalar.copy(out=out, in_=in_)
+
+        bps = ps_tr.tile([P, P], BF16, name="bps", tag="tr")
+        nc.tensor.transpose(bps[:], brow[:], ident_b[:])
+        bcol = keep.tile([P, 16], F32, name="bcol")
+        nc.vector.tensor_copy(out=bcol[:], in_=bps[:, 0:16])
+        bsum = keep.tile([P, 8], F32, name="bsum")
+        nc.vector.tensor_tensor(out=bsum[:], in0=bcol[:, 0:8], in1=bcol[:, 8:16], op=ALU.add)
+
+        def turn(words, base, g, dst):
+            for u in (0, 1):
+                nc.tensor.transpose(dst[:, u, :], words[:, base + 256 * g + u : base + 256 * (g + 1) : 2], ident_f[:])
+
+        hgrp = {}
+
+        def h_turn(a, q, g, engs):
+            words = h_sb[(a, q)][:].rearrange("p k d -> p (k d)").bitcast(F32)
+            grp = hst.tile([P, 4 * P * 4], BF16, name="hgrp", tag="hgrp", align_bytes=64)
+            hgrp[(a, q, g)] = grp
+            gw = grp[:].bitcast(F32).rearrange("p (k n u) -> p k n u", k=4, u=2)
+            for pr in (0, 1):
+                tr = ps_tr.tile([P, 2, 2, P], F32, name="tr", tag="tr")
+                for i in (0, 1):
+                    turn(words, 512 * (2 * pr + i), g, tr[:, i, :, :])
+                copy_on(engs[pr], gw[:, 2 * pr : 2 * pr + 2, :, :], tr[:].rearrange("p i u n -> p i n u"))
+
+        def h_quant(a, q, g):
+            cols = slice(512 * q, 512 * (q + 1))
+            nc.vector.quantize_mx(
+                out=h_codes[:, a, g, cols].bitcast(FP8X4), scales=h_scales[:, a, g, cols], in_=hgrp[(a, q, g)][:]
+            )
+
+        xgrp = {}
+
+        def x_turn(g, eng):
+            words = x_sb[:].rearrange("p a d -> p (a d)").bitcast(F32)
+            grp = hst.tile([P, NODES * 4], BF16, name="xgrp", tag="xgrp", align_bytes=64)
+            xgrp[g] = grp
+            tr = ps_tr.tile([P, 2, 2, P], F32, name="tr", tag="tr")
+            for a in (0, 1):
+                turn(words, 512 * a, g, tr[:, a, :, :])
+            copy_on(eng, grp[:].bitcast(F32).rearrange("p (a n u) -> p a n u", a=2, u=2), tr[:].rearrange("p a u n -> p a n u"))
+
+        def x_quant(g):
+            nc.vector.quantize_mx(out=x_codes[:, g, :].bitcast(FP8X4), scales=x_scales[:, g, :], in_=xgrp[g][:])
+
+        wgrp = {}
+
+        def w_copy(m, g, sc, eng):
+            raw = wraw[(m, g, min(sc, 2))]
+            off = 256 if sc == 3 else 0
+            grp = wst.tile([P, 256, 4], BF16, name="wgrp", tag="wgrp", align_bytes=64)
+            wgrp[(m, g, sc)] = grp
+            copy_on(eng, grp[:], raw[:, :, off : off + 256].rearrange("p t w -> p w t"))
+
+        def w_quant(m, g, sc):
+            cols = slice(256 * sc, 256 * (sc + 1))
+            nc.vector.quantize_mx(
+                out=w_codes[:, m, g, cols].bitcast(FP8X4),
+                scales=w_scales[:, m, g, cols],
+                in_=wgrp[(m, g, sc)][:].rearrange("p w t -> p (w t)"),
+            )
+
+        def xf(sc):
+            ps = ps_tr.tile([P, 2, NODES], F32, name="xps", tag="tr")
+            for jj in (0, 1):
+                cols = slice(P * (2 * sc + jj), P * (2 * sc + jj + 1))
+                for g in (0, 1):
+                    nc.tensor.matmul_mx(
+                        out=ps[:, jj, :],
+                        lhsT=w_codes[:, 0, g, cols].bitcast(FP8X4),
+                        lhsT_scale=w_scales[:, 0, g, cols],
+                        rhs=x_codes[:, g, :].bitcast(FP8X4),
+                        rhs_scale=x_scales[:, g, :],
+                        start=(g == 0),
+                        stop=(g == 1),
+                    )
+            for jj in (0, 1):
+                j = 2 * sc + jj
+                nc.scalar.activation(out=xfT[:, j, :], in_=ps[:, jj, :], func=ACT.Identity, bias=bsum[:, j : j + 1], scale=1.0)
+
+        steps = [(a, 4 * hh + jq) for hh in (0, 1) for a in (0, 1) for jq in range(4)]
+        NS = len(steps)
+        z_t, ct_t, zz_t, f_t, p_t, o_t = {}, {}, {}, {}, {}, {}
+
+        def mx(s, q):
+            a, j = steps[s]
+            z = ps_z.tile([P, 512], F32, name="z", tag="z")
+            z_t[(s, q)] = z
+            jc = slice(P * j, P * (j + 1))
+            qc = slice(512 * q, 512 * (q + 1))
+            for g in (0, 1):
+                nc.tensor.matmul_mx(
+                    out=z[:],
+                    lhsT=w_codes[:, 1, g, jc].bitcast(FP8X4),
+                    lhsT_scale=w_scales[:, 1, g, jc],
+                    rhs=h_codes[:, a, g, qc].bitcast(FP8X4),
+                    rhs_scale=h_scales[:, a, g, qc],
+                    start=(g == 0),
+                    stop=(g == 1),
+                )
+
+        def ct(s):
+            a, j = steps[s]
+            t = ps_ct.tile([P, KIDS, P], BF16, name="ct", tag="ct")
+            ct_t[s] = t
+            for k in range(KIDS):
+                nc.tensor.transpose(t[:, k, :], c_block(a, j, k), ident_b[:])
+
+        def add_x(s, q):
+            a, j = steps[s]
+            zz = zzp.tile([P, 512], F32, name="zz", tag="zz")
+            zz_t[(s, q)] = zz
+            nc.vector.tensor_tensor(
+                out=zz[:].rearrange("p (k n) -> p k n", k=4),
+                in0=z_t[(s, q)][:].rearrange("p (k n) -> p k n", k=4),
+                in1=xfT[:, j, P * a : P * (a + 1)].unsqueeze(1).to_broadcast([P, 4, P]),
+                op=ALU.add,
+            )
+
+        def gate(s, q):
+            f = fpl.tile([P, 512], F32, name="f", tag="f")
+            f_t[(s, q)] = f
+            nc.scalar.activation(out=f[:], in_=zz_t[(s, q)][:], func=ACT.Sigmoid)
+
+        def times_c(s, q):
+            p = ppl.tile([P, 512], F32, name="p", tag="p")
+            p_t[(s, q)] = p
+            nc.vector.tensor_tensor(
+                out=p[:],
+                in0=f_t[(s, q)][:],
+                in1=ct_t[s][:, 4 * q : 4 * q + 4, :].rearrange("p k n -> p (k n)"),
+                op=ALU.mult,
+            )
+
+        def add_up(s, q):
+            if q == 0:
+                o = ps_o.tile([P, P], F32, name="o", tag="o")
+                o_t[s] = o
+            for kk in range(4):
+                nc.tensor.matmul(
+                    out=o_t[s][:],
+                    lhsT=p_t[(s, q)][:, P * kk : P * (kk + 1)],
+                    rhs=ident_f[:],
+                    is_transpose=True,
+                    start=(q == 0 and kk == 0),
+                    stop=(q == 1 and kk == 3),
+                )
+
+        def leave(s):
+            a, j = steps[s]
+            nc.scalar.copy(out=out_sb[:, a, P * j : P * (j + 1)], in_=o_t[s][:])
+            if j % 2 == 1:
+                cols = slice(P * (j - 1), P * (j + 1))
+                nc.sync.dma_start(out=out_0[P * a : P * (a + 1), cols], in_=out_sb[:, a, cols])
+                nc.vector.tensor_reduce(
+                    out=stats[:, s // 2 : s // 2 + 1], in_=out_sb[:, a, cols], axis=AX.X, op=ALU.max, apply_absolute_value=True
+                )
+
+        h_turn(0, 0, 0, "vs")
+        h_turn(0, 0, 1, "vs")
+        x_turn(0, "v")
+        x_turn(1, "s")
+        h_quant(0, 0, 0)
+        h_quant(0, 0, 1)
+        x_quant(0)
+        x_quant(1)
+        w_copy(0, 0, 0, "v")
+        w_copy(0, 1, 0, "s")
+        w_copy(1, 0, 0, "v")
+        w_copy(1, 1, 0, "s")
+        w_quant(0, 0, 0)
+        w_quant(0, 1, 0)
+        xf(0)
+        w_quant(1, 0, 0)
+        w_quant(1, 1, 0)
+        mx(0, 0)
+        h_turn(0, 1, 0, "vs")
+        h_turn(0, 1, 1, "vs")
+        h_quant(0, 1, 0)
+        h_quant(0, 1, 1)
+        mx(0, 1)
+
+        def extras(s):
+            if s == 0:
+                w_copy(0, 0, 1, "v")
+                w_copy(0, 1, 1, "s")
+                w_quant(0, 0, 1)
+                w_quant(0, 1, 1)
+                w_copy(1, 0, 1, "v")
+                w_copy(1, 1, 1, "s")
+            if s == 1:
+                xf(1)
+                w_quant(1, 0, 1)
+                w_quant(1, 1, 1)
+            if s in (2, 3):
+                h_turn(1, s - 2, 0, "sv")
+                h_turn(1, s - 2, 1, "sv")
+                h_quant(1, s - 2, 0)
+                h_quant(1, s - 2, 1)
+            if s == 4:
+                w_copy(0, 0, 2, "s")
+            if s == 5:
+                w_quant(0, 0, 2)
+                w_copy(0, 1, 2, "s")
+                w_copy(1, 0, 2, "v")
+            if s == 6:
+                w_quant(0, 1, 2)
+                w_quant(1, 0, 2)
+                w_copy(1, 1, 2, "s")
+                xf(2)
+            if s == 7:
+                w_quant(1, 1, 2)
+                w_copy(0, 0, 3, "s")
+            if s == 8:
+                w_quant(0, 0, 3)
+                w_copy(0, 1, 3, "s")
+                w_copy(1, 0, 3, "v")
+            if s == 9:
+                w_quant(0, 1, 3)
+                w_quant(1, 0, 3)
+                w_copy(1, 1, 3, "s")
+                xf(3)
+                w_quant(1, 1, 3)
+
+        for s in range(NS + 1):
+            if s < NS:
+                ct(s)
+            if s >= 1:
+                times_c(s - 1, 0)
+            if s < NS:
+                add_x(s, 0)
+                gate(s, 0)
+            if s >= 1:
+                add_up(s - 1, 0)
+                times_c(s - 1, 1)
+            if s < NS:
+                add_x(s, 1)
+                gate(s, 1)
+            if s >= 1:
+                add_up(s - 1, 1)
+                leave(s - 1)
+            extras(s)
+            if s + 1 < NS:
+                mx(s + 1, 0)
+                mx(s + 1, 1)
+
+        pmax = keep.tile([P, 1], F32, name="pmax")
+        nc.vector.tensor_reduce(out=pmax[:], in_=stats[:], axis=AX.X, op=ALU.max)
+        aps = ps_tr.tile([P, P], F32, name="aps", tag="tr")
+        nc.tensor.transpose(aps[:], pmax[:, 0:1].to_broadcast([P, P]), ident_f[:])
+        amax = keep.tile([P, 1], F32, name="amax")
+        nc.vector.tensor_reduce(out=amax[:], in_=aps[:], axis=AX.X, op=ALU.max)
+        rec = keep.tile([P, 1], F32, name="rec")
+        nc.vector.reciprocal(out=rec[:], in_=amax[:])
+        fac = keep.tile([P, 1], F32, name="fac")
+        nc.vector.tensor_scalar(out=fac[:], in0=rec[:], scalar1=448.0, scalar2=None, op0=ALU.mult)
+
+        o8a = keep.tile([P, H], FP8, name="o8a")
+        o8b = keep.tile([P, H], FP8, name="o8b")
+        nc.vector.tensor_scalar(out=o8a[:], in0=out_sb[:, 0, :], scalar1=fac[:, 0:1], scalar2=None, op0=ALU.mult, saturate=False)
+        nc.scalar.activation(
+            out=o8b[:], in_=out_sb[:, 1, :], func=ACT.Identity, scale=fac[:, 0:1], bias=zero_col[:, 0:1], saturate=False
+        )
+        nc.sync.dma_start(out=out_1[0:P, :], in_=o8a[:].bitcast(U8))
+        nc.sync.dma_start(out=out_1[P : 2 * P, :], in_=o8b[:].bitcast(U8))

@@ -26,69 +26,62 @@ def tile_childsumtreelstmcell_pa_kernel(tc, x, child_h, child_c, Wf, bWf, Uf, bU
         hst = ctx.enter_context(tc.tile_pool(name="hst", bufs=3))
         zzp = ctx.enter_context(tc.tile_pool(name="zzp", bufs=3))
         fpl = ctx.enter_context(tc.tile_pool(name="fpl", bufs=4))
-        ppl = ctx.enter_context(tc.tile_pool(name="ppl", bufs=4))
+        ppl = ctx.enter_context(tc.tile_pool(name="ppl", bufs=10))
+        pap = ctx.enter_context(tc.tile_pool(name="pap", bufs=4))
         ps_z = ctx.enter_context(tc.psum_pool(name="ps_z", bufs=3))
         ps_ct = ctx.enter_context(tc.psum_pool(name="ps_ct", bufs=2))
-        ps_tr = ctx.enter_context(tc.psum_pool(name="ps_tr", bufs=2))
-        ps_o = ctx.enter_context(tc.psum_pool(name="ps_o", bufs=1))
+        ps_tr = ctx.enter_context(tc.psum_pool(name="ps_tr", bufs=3))
+        ctx.enter_context(tc.manual_schedule())
 
         ident_f = keep.tile([P, P], F32, name="ident_f")
         make_identity(nc, ident_f[:])
-        ident_b = keep.tile([P, P], BF16, name="ident_b")
-        make_identity(nc, ident_b[:])
         zero_col = keep.tile([P, 1], F32, name="zero_col")
         nc.vector.memset(zero_col[:], 0.0)
         warm = keep.tile([P, 1], F32, name="warm")
         nc.scalar.activation(out=warm[:], in_=zero_col[:], func=ACT.Sigmoid)
-        brow = keep.tile([P, P], BF16, name="brow")
+        brow = keep.tile([P, 2 * P], BF16, name="brow")
         nc.vector.memset(brow[:], 0.0)
-        nc.scalar.dma_start(out=brow[0:8, :], in_=bWf.rearrange("(j p) -> j p", p=P))
-        nc.scalar.dma_start(out=brow[8:16, :], in_=bUf.rearrange("(j p) -> j p", p=P))
+        nc.scalar.dma_start(out=brow[0:4, :], in_=bWf.rearrange("(r c) -> r c", c=2 * P))
+        nc.scalar.dma_start(out=brow[4:8, :], in_=bUf.rearrange("(r c) -> r c", c=2 * P))
 
         def load(name, shape, src):
             t = keep.tile(shape, BF16, name=name)
             nc.sync.dma_start(out=t[:], in_=src)
             return t
 
-        def load_w(m, g, c0, c1):
-            src = (Wf, Uf)[m][512 * g : 512 * (g + 1), c0:c1].rearrange("(p t) w -> p t w", t=4)
-            return load("wraw%d_%d_%d" % (m, g, c0), [P, 4, c1 - c0], src)
+        wraw, h_sb, c_sb = {}, {}, {}
+
+        def load_w(m, hh):
+            for g in (0, 1):
+                src = (Wf, Uf)[m][512 * g : 512 * (g + 1), 512 * hh : 512 * (hh + 1)].rearrange("(p t) w -> p t w", t=4)
+                wraw[(m, g, hh)] = load("wraw%d_%d_%d" % (m, g, hh), [P, 4, 512], src)
 
         def load_h(a, q):
-            return load("h%d_%d" % (a, q), [P, 4, D], child_h[P * a : P * (a + 1), 4 * q : 4 * q + 4, :])
+            for i in (0, 1):
+                k0 = 4 * q + 2 * i
+                h_sb[(a, q, i)] = load("h%d_%d_%d" % (a, q, i), [P, 2, D], child_h[P * a : P * (a + 1), k0 : k0 + 2, :])
 
-        def load_c(a, c0, c1):
-            return load("c%d_%d" % (a, c0), [P, KIDS, c1 - c0], child_c[P * a : P * (a + 1), :, c0:c1])
+        def load_c(a, q, hh):
+            src = child_c[P * a : P * (a + 1), 4 * q : 4 * q + 4, 512 * hh : 512 * (hh + 1)]
+            c_sb[(a, q, hh)] = load("c%d_%d_%d" % (a, q, hh), [P, 4, 512], src)
 
-        wraw = {}
-        h_sb = {}
-        c_sb = {}
-        h_sb[(0, 0)] = load_h(0, 0)
+        load_h(0, 0)
         x_sb = load("x_sb", [P, 2, D], x.rearrange("(a p) d -> p a d", p=P))
-        for m in (0, 1):
-            for g in (0, 1):
-                wraw[(m, g, 0)] = load_w(m, g, 0, 256)
-        h_sb[(0, 1)] = load_h(0, 1)
-        c_sb[(0, 0)] = load_c(0, 0, 256)
-        for m in (0, 1):
-            for g in (0, 1):
-                wraw[(m, g, 1)] = load_w(m, g, 256, 512)
-        c_sb[(0, 1)] = load_c(0, 256, 512)
-        h_sb[(1, 0)] = load_h(1, 0)
-        h_sb[(1, 1)] = load_h(1, 1)
-        c_sb[(1, 0)] = load_c(1, 0, 512)
-        for m in (0, 1):
-            for g in (0, 1):
-                wraw[(m, g, 2)] = load_w(m, g, 512, 1024)
-        c_sb[(0, 2)] = load_c(0, 512, 1024)
-        c_sb[(1, 2)] = load_c(1, 512, 1024)
-
-        def c_block(a, j, k):
-            if j >= 4:
-                return c_sb[(a, 2)][:, k, P * (j - 4) : P * (j - 3)]
-            if a == 1:
-                return c_sb[(1, 0)][:, k, P * j : P * (j + 1)]
-            return c_sb[(0, j // 2)][:, k, P * (j % 2) : P * (j % 2 + 1)]
+        load_w(0, 0)
+        load_w(1, 0)
+        load_h(0, 1)
+        load_c(0, 0, 0)
+        load_h(1, 0)
+        load_c(0, 1, 0)
+        load_h(1, 1)
+        load_c(1, 0, 0)
+        load_w(0, 1)
+        load_c(1, 1, 0)
+        load_w(1, 1)
+        load_c(0, 0, 1)
+        load_c(0, 1, 1)
+        load_c(1, 0, 1)
+        load_c(1, 1, 1)
 
         w_codes = keep.tile([P, 2, 2, H], U32, name="w_codes", align_bytes=64)
         w_scales = keep.tile([P, 2, 2, H], U8, name="w_scales", align_bytes=64)
@@ -99,36 +92,42 @@ def tile_childsumtreelstmcell_pa_kernel(tc, x, child_h, child_c, Wf, bWf, Uf, bU
         xfT = keep.tile([P, 8, NODES], F32, name="xfT")
         out_sb = keep.tile([P, 2, H], F32, name="out_sb")
         stats = keep.tile([P, 8], F32, name="stats")
+        bcol = keep.tile([P, 16], F32, name="bcol")
+        bsum = keep.tile([P, 8], F32, name="bsum")
 
         def copy_on(eng, out, in_):
             if eng == "v":
                 nc.vector.tensor_copy(out=out, in_=in_)
-            else:
+            elif eng == "s":
                 nc.scalar.copy(out=out, in_=in_)
+            else:
+                nc.gpsimd.tensor_scalar(out=out, in0=in_, scalar1=1.0, scalar2=0.0, op0=ALU.mult, op1=ALU.add)
 
-        bps = ps_tr.tile([P, P], BF16, name="bps", tag="tr")
-        nc.tensor.transpose(bps[:], brow[:], ident_b[:])
-        bcol = keep.tile([P, 16], F32, name="bcol")
-        nc.vector.tensor_copy(out=bcol[:], in_=bps[:, 0:16])
-        bsum = keep.tile([P, 8], F32, name="bsum")
-        nc.vector.tensor_tensor(out=bsum[:], in0=bcol[:, 0:8], in1=bcol[:, 8:16], op=ALU.add)
+        def bias():
+            bps = ps_tr.tile([P, P], F32, name="bps", tag="tr")
+            nc.tensor.transpose(bps[:], brow[:].bitcast(F32), ident_f[:])
+            nc.vector.tensor_copy(out=bcol[:], in_=bps[:, 0:8].bitcast(BF16))
+            nc.vector.tensor_tensor(out=bsum[:], in0=bcol[:, 0:8], in1=bcol[:, 8:16], op=ALU.add)
 
         def turn(words, base, g, dst):
             for u in (0, 1):
                 nc.tensor.transpose(dst[:, u, :], words[:, base + 256 * g + u : base + 256 * (g + 1) : 2], ident_f[:])
 
-        hgrp = {}
+        hgrp, htr = {}, {}
 
-        def h_turn(a, q, g, engs):
-            words = h_sb[(a, q)][:].rearrange("p k d -> p (k d)").bitcast(F32)
-            grp = hst.tile([P, 4 * P * 4], BF16, name="hgrp", tag="hgrp", align_bytes=64)
-            hgrp[(a, q, g)] = grp
-            gw = grp[:].bitcast(F32).rearrange("p (k n u) -> p k n u", k=4, u=2)
-            for pr in (0, 1):
-                tr = ps_tr.tile([P, 2, 2, P], F32, name="tr", tag="tr")
-                for i in (0, 1):
-                    turn(words, 512 * (2 * pr + i), g, tr[:, i, :, :])
-                copy_on(engs[pr], gw[:, 2 * pr : 2 * pr + 2, :, :], tr[:].rearrange("p i u n -> p i n u"))
+        def h_tr(a, q, g, i):
+            words = h_sb[(a, q, i)][:].rearrange("p k d -> p (k d)").bitcast(F32)
+            tr = ps_tr.tile([P, 2, 2, P], F32, name="tr", tag="tr")
+            htr[(a, q, g, i)] = tr
+            for kk in (0, 1):
+                turn(words, 512 * kk, g, tr[:, kk, :, :])
+
+        def h_cp(a, q, g, i, eng):
+            if i == 0:
+                grp = hst.tile([P, 4 * P * 4], BF16, name="hgrp", tag="hgrp", align_bytes=64)
+                hgrp[(a, q, g)] = grp
+            gw = hgrp[(a, q, g)][:].bitcast(F32).rearrange("p (k n u) -> p k n u", k=4, u=2)
+            copy_on(eng, gw[:, 2 * i : 2 * i + 2, :, :], htr[(a, q, g, i)][:].rearrange("p i u n -> p i n u"))
 
         def h_quant(a, q, g):
             cols = slice(512 * q, 512 * (q + 1))
@@ -152,23 +151,28 @@ def tile_childsumtreelstmcell_pa_kernel(tc, x, child_h, child_c, Wf, bWf, Uf, bU
 
         wgrp = {}
 
-        def w_copy(m, g, sc, eng):
-            raw = wraw[(m, g, min(sc, 2))]
-            off = 256 if sc == 3 else 0
-            grp = wst.tile([P, 256, 4], BF16, name="wgrp", tag="wgrp", align_bytes=64)
-            wgrp[(m, g, sc)] = grp
-            copy_on(eng, grp[:], raw[:, :, off : off + 256].rearrange("p t w -> p w t"))
-
-        def w_quant(m, g, sc):
-            cols = slice(256 * sc, 256 * (sc + 1))
-            nc.vector.quantize_mx(
-                out=w_codes[:, m, g, cols].bitcast(FP8X4),
-                scales=w_scales[:, m, g, cols],
-                in_=wgrp[(m, g, sc)][:].rearrange("p w t -> p (w t)"),
+        def w_copy(m, g, c0, c1, eng):
+            raw = wraw[(m, g, c0 // 512)]
+            grp = wst.tile([P, c1 - c0, 4], BF16, name="wgrp", tag="wgrp", align_bytes=64)
+            wgrp[(m, g, c0)] = grp
+            copy_on(
+                eng,
+                grp[:].rearrange("p (b m) t -> p b m t", b=2),
+                raw[:, :, c0 % 512 : c0 % 512 + c1 - c0].rearrange("p t (m b) -> p b m t", b=2),
             )
 
-        def xf(sc):
+        def w_quant(m, g, c0, c1):
+            nc.vector.quantize_mx(
+                out=w_codes[:, m, g, c0:c1].bitcast(FP8X4),
+                scales=w_scales[:, m, g, c0:c1],
+                in_=wgrp[(m, g, c0)][:].rearrange("p w t -> p (w t)"),
+            )
+
+        xps = {}
+
+        def xf_mm(sc):
             ps = ps_tr.tile([P, 2, NODES], F32, name="xps", tag="tr")
+            xps[sc] = ps
             for jj in (0, 1):
                 cols = slice(P * (2 * sc + jj), P * (2 * sc + jj + 1))
                 for g in (0, 1):
@@ -181,175 +185,233 @@ def tile_childsumtreelstmcell_pa_kernel(tc, x, child_h, child_c, Wf, bWf, Uf, bU
                         start=(g == 0),
                         stop=(g == 1),
                     )
+
+        def xf_ev(sc):
             for jj in (0, 1):
                 j = 2 * sc + jj
-                nc.scalar.activation(out=xfT[:, j, :], in_=ps[:, jj, :], func=ACT.Identity, bias=bsum[:, j : j + 1], scale=1.0)
+                nc.scalar.activation(out=xfT[:, j, :], in_=xps[sc][:, jj, :], func=ACT.Identity, bias=bsum[:, j : j + 1], scale=1.0)
 
-        steps = [(a, 4 * hh + jq) for hh in (0, 1) for a in (0, 1) for jq in range(4)]
+        steps = [(a, q, jp) for a in (0, 1) for q in (0, 1) for jp in (0, 1)]
+        steps += [(a, q, jp) for a in (0, 1) for jp in (2, 3) for q in (0, 1)]
         NS = len(steps)
         z_t, ct_t, zz_t, f_t, p_t, o_t = {}, {}, {}, {}, {}, {}
 
-        def mx(s, q):
-            a, j = steps[s]
-            z = ps_z.tile([P, 512], F32, name="z", tag="z")
-            z_t[(s, q)] = z
-            jc = slice(P * j, P * (j + 1))
+        def mx(s, bs=(0, 1)):
+            a, q, jp = steps[s]
             qc = slice(512 * q, 512 * (q + 1))
-            for g in (0, 1):
-                nc.tensor.matmul_mx(
-                    out=z[:],
-                    lhsT=w_codes[:, 1, g, jc].bitcast(FP8X4),
-                    lhsT_scale=w_scales[:, 1, g, jc],
-                    rhs=h_codes[:, a, g, qc].bitcast(FP8X4),
-                    rhs_scale=h_scales[:, a, g, qc],
-                    start=(g == 0),
-                    stop=(g == 1),
-                )
+            for b in bs:
+                z = ps_z.tile([P, 512], F32, name="z", tag="z")
+                z_t[(s, b)] = z
+                jc = slice(P * (2 * jp + b), P * (2 * jp + b + 1))
+                for g in (0, 1):
+                    nc.tensor.matmul_mx(
+                        out=z[:],
+                        lhsT=w_codes[:, 1, g, jc].bitcast(FP8X4),
+                        lhsT_scale=w_scales[:, 1, g, jc],
+                        rhs=h_codes[:, a, g, qc].bitcast(FP8X4),
+                        rhs_scale=h_scales[:, a, g, qc],
+                        start=(g == 0),
+                        stop=(g == 1),
+                    )
 
         def ct(s):
-            a, j = steps[s]
-            t = ps_ct.tile([P, KIDS, P], BF16, name="ct", tag="ct")
+            a, q, jp = steps[s]
+            t = ps_ct.tile([P, 4, P], F32, name="ct", tag="ct")
             ct_t[s] = t
-            for k in range(KIDS):
-                nc.tensor.transpose(t[:, k, :], c_block(a, j, k), ident_b[:])
+            src = c_sb[(a, q, jp // 2)]
+            c0 = 256 * (jp % 2)
+            for kk in range(4):
+                nc.tensor.transpose(t[:, kk, :], src[:, kk, c0 : c0 + 256].bitcast(F32), ident_f[:])
 
-        def add_x(s, q):
-            a, j = steps[s]
+        def add_x(s, b):
+            a, q, jp = steps[s]
             zz = zzp.tile([P, 512], F32, name="zz", tag="zz")
-            zz_t[(s, q)] = zz
+            zz_t[(s, b)] = zz
             nc.vector.tensor_tensor(
                 out=zz[:].rearrange("p (k n) -> p k n", k=4),
-                in0=z_t[(s, q)][:].rearrange("p (k n) -> p k n", k=4),
-                in1=xfT[:, j, P * a : P * (a + 1)].unsqueeze(1).to_broadcast([P, 4, P]),
+                in0=z_t[(s, b)][:].rearrange("p (k n) -> p k n", k=4),
+                in1=xfT[:, 2 * jp + b, P * a : P * (a + 1)].unsqueeze(1).to_broadcast([P, 4, P]),
                 op=ALU.add,
             )
 
-        def gate(s, q):
+        def gate(s, b):
             f = fpl.tile([P, 512], F32, name="f", tag="f")
-            f_t[(s, q)] = f
-            nc.scalar.activation(out=f[:], in_=zz_t[(s, q)][:], func=ACT.Sigmoid)
+            f_t[(s, b)] = f
+            nc.scalar.activation(out=f[:], in_=zz_t[(s, b)][:], func=ACT.Sigmoid)
 
-        def times_c(s, q):
+        def times_c(s, b):
+            a, q, jp = steps[s]
             p = ppl.tile([P, 512], F32, name="p", tag="p")
-            p_t[(s, q)] = p
+            p_t[(a, q, jp, b)] = p
             nc.vector.tensor_tensor(
                 out=p[:],
-                in0=f_t[(s, q)][:],
-                in1=ct_t[s][:, 4 * q : 4 * q + 4, :].rearrange("p k n -> p (k n)"),
+                in0=f_t[(s, b)][:],
+                in1=ct_t[s][:].rearrange("p k n -> p (k n)").bitcast(BF16).rearrange("p (x e) -> p x e", e=2)[:, :, b],
                 op=ALU.mult,
             )
 
-        def add_up(s, q):
-            if q == 0:
-                o = ps_o.tile([P, P], F32, name="o", tag="o")
-                o_t[s] = o
-            for kk in range(4):
-                nc.tensor.matmul(
-                    out=o_t[s][:],
-                    lhsT=p_t[(s, q)][:, P * kk : P * (kk + 1)],
-                    rhs=ident_f[:],
-                    is_transpose=True,
-                    start=(q == 0 and kk == 0),
-                    stop=(q == 1 and kk == 3),
-                )
+        def add_up(s, bs=(0, 1)):
+            a, q, jp = steps[s]
+            if 0 in bs:
+                o_new = ps_tr.tile([P, 2, P], F32, name="o", tag="tr")
+                o_t[s] = o_new
+            o = o_t[s]
+            for b in bs:
+                srcs = [pa_t[(a, jp, b)]] if (a, jp, b) in pa_t else [p_t[(a, 0, jp, b)], p_t[(a, 1, jp, b)]]
+                for n, src in enumerate(srcs):
+                    for kk in range(4):
+                        nc.tensor.matmul(
+                            out=o[:, b, :],
+                            lhsT=src[:, P * kk : P * (kk + 1)],
+                            rhs=ident_f[:],
+                            is_transpose=True,
+                            start=(n == 0 and kk == 0),
+                            stop=(n == len(srcs) - 1 and kk == 3),
+                        )
+
+        pa_t = {}
+
+        def pre_add(s):
+            a, q, jp = steps[s]
+            for b in (0, 1):
+                t = pap.tile([P, 512], F32, name="pa", tag="pa")
+                pa_t[(a, jp, b)] = t
+                nc.gpsimd.tensor_tensor(out=t[:], in0=p_t[(a, 0, jp, b)][:], in1=p_t[(a, 1, jp, b)][:], op=ALU.add)
+
+        n_done = [0]
 
         def leave(s):
-            a, j = steps[s]
-            nc.scalar.copy(out=out_sb[:, a, P * j : P * (j + 1)], in_=o_t[s][:])
-            if j % 2 == 1:
-                cols = slice(P * (j - 1), P * (j + 1))
-                nc.sync.dma_start(out=out_0[P * a : P * (a + 1), cols], in_=out_sb[:, a, cols])
-                nc.vector.tensor_reduce(
-                    out=stats[:, s // 2 : s // 2 + 1], in_=out_sb[:, a, cols], axis=AX.X, op=ALU.max, apply_absolute_value=True
-                )
+            a, q, jp = steps[s]
+            cols = slice(256 * jp, 256 * (jp + 1))
+            nc.scalar.copy(out=out_sb[:, a, cols].rearrange("p (m b) -> p m b", b=2), in_=o_t[s][:].rearrange("p b m -> p m b"))
+            nc.sync.dma_start(out=out_0[P * a : P * (a + 1), cols], in_=out_sb[:, a, cols])
 
-        h_turn(0, 0, 0, "vs")
-        h_turn(0, 0, 1, "vs")
-        x_turn(0, "v")
-        x_turn(1, "s")
+        def peak(s):
+            a, q, jp = steps[s]
+            cols = slice(256 * jp, 256 * (jp + 1))
+            i = n_done[0]
+            n_done[0] = i + 1
+            nc.vector.tensor_reduce(out=stats[:, i : i + 1], in_=out_sb[:, a, cols], axis=AX.X, op=ALU.max, apply_absolute_value=True)
+
+        for i in (0, 1):
+            h_tr(0, 0, 0, i)
+            h_cp(0, 0, 0, i, "v")
+            h_tr(0, 0, 1, i)
+            h_cp(0, 0, 1, i, "s")
         h_quant(0, 0, 0)
+        x_turn(0, "s")
+        x_turn(1, "s")
+        bias()
         h_quant(0, 0, 1)
+        w_copy(0, 0, 0, 256, "v")
+        w_copy(0, 0, 256, 512, "s")
         x_quant(0)
+        w_quant(0, 0, 0, 256)
         x_quant(1)
-        w_copy(0, 0, 0, "v")
-        w_copy(0, 1, 0, "s")
-        w_copy(1, 0, 0, "v")
-        w_copy(1, 1, 0, "s")
-        w_quant(0, 0, 0)
-        w_quant(0, 1, 0)
-        xf(0)
-        w_quant(1, 0, 0)
-        w_quant(1, 1, 0)
-        mx(0, 0)
-        h_turn(0, 1, 0, "vs")
-        h_turn(0, 1, 1, "vs")
-        h_quant(0, 1, 0)
-        h_quant(0, 1, 1)
-        mx(0, 1)
+        w_copy(0, 1, 0, 256, "v")
+        w_copy(0, 1, 256, 512, "s")
+        w_quant(0, 0, 256, 512)
+        w_quant(0, 1, 0, 256)
+        xf_mm(0)
+        w_copy(1, 0, 0, 256, "v")
+        w_copy(1, 0, 256, 512, "s")
+        w_quant(0, 1, 256, 512)
+        xf_mm(1)
+        w_quant(1, 0, 0, 256)
+        xf_ev(0)
+        w_copy(1, 1, 0, 256, "v")
+        w_copy(1, 1, 256, 512, "s")
+        w_quant(1, 0, 256, 512)
+        w_quant(1, 1, 0, 256)
+        mx(0)
+        xf_ev(1)
+        w_quant(1, 1, 256, 512)
+        for g in (0, 1):
+            for i in (0, 1):
+                h_tr(0, 1, g, i)
+                h_cp(0, 1, g, i, "s")
 
-        def extras(s):
+        HT = {1: (1, 0), 2: (1, 1)}
+        CP = {5: (0, 512), 6: (0, 768), 7: (1, 512), 8: (1, 768)}
+        QU = {6: (0, 512), 7: (0, 768), 8: (1, 768)}
+        QM = {7: (1, 512)}
+        XF = {6: 2, 7: 3}
+
+        def t_extra(s):
+            if s in HT:
+                a, q = HT[s]
+                for g in (0, 1):
+                    for i in (0, 1):
+                        h_tr(a, q, g, i)
+                        h_cp(a, q, g, i, "s")
+            if s in XF:
+                xf_mm(XF[s])
+                xf_ev(XF[s])
+
+        def s_extra(s):
+            if s in CP:
+                m, c0 = CP[s]
+                w_copy(m, 0, c0, c0 + 256, "s")
+                w_copy(m, 1, c0, c0 + 256, "g")
+
+        def v_extra(s):
             if s == 0:
-                w_copy(0, 0, 1, "v")
-                w_copy(0, 1, 1, "s")
-                w_quant(0, 0, 1)
-                w_quant(0, 1, 1)
-                w_copy(1, 0, 1, "v")
-                w_copy(1, 1, 1, "s")
-            if s == 1:
-                xf(1)
-                w_quant(1, 0, 1)
-                w_quant(1, 1, 1)
-            if s in (2, 3):
-                h_turn(1, s - 2, 0, "sv")
-                h_turn(1, s - 2, 1, "sv")
-                h_quant(1, s - 2, 0)
-                h_quant(1, s - 2, 1)
-            if s == 4:
-                w_copy(0, 0, 2, "s")
-            if s == 5:
-                w_quant(0, 0, 2)
-                w_copy(0, 1, 2, "s")
-                w_copy(1, 0, 2, "v")
-            if s == 6:
-                w_quant(0, 1, 2)
-                w_quant(1, 0, 2)
-                w_copy(1, 1, 2, "s")
-                xf(2)
-            if s == 7:
-                w_quant(1, 1, 2)
-                w_copy(0, 0, 3, "s")
-            if s == 8:
-                w_quant(0, 0, 3)
-                w_copy(0, 1, 3, "s")
-                w_copy(1, 0, 3, "v")
-            if s == 9:
-                w_quant(0, 1, 3)
-                w_quant(1, 0, 3)
-                w_copy(1, 1, 3, "s")
-                xf(3)
-                w_quant(1, 1, 3)
+                h_quant(0, 1, 0)
+                h_quant(0, 1, 1)
+            if s - 1 in HT:
+                a, q = HT[s - 1]
+                h_quant(a, q, 0)
+                h_quant(a, q, 1)
+            if s in QU:
+                m, c0 = QU[s]
+                w_quant(m, 0, c0, c0 + 256)
+                w_quant(m, 1, c0, c0 + 256)
 
-        for s in range(NS + 1):
-            if s < NS:
-                ct(s)
-            if s >= 1:
-                times_c(s - 1, 0)
+        def is_last_q(s):
+            return 0 <= s < NS and steps[s][1] == 1
+
+        todo = []
+        left = []
+        seen = []
+        for s in range(NS + 4):
+            late = s in QM
+            if s + 1 < NS and not late:
+                mx(s + 1, (0,))
+            if left:
+                leave(left[0])
+                seen.append(left[0])
+                left.remove(left[0])
+            s_extra(s)
             if s < NS:
                 add_x(s, 0)
                 gate(s, 0)
-            if s >= 1:
-                add_up(s - 1, 0)
-                times_c(s - 1, 1)
+            if s + 1 < NS and not late:
+                mx(s + 1, (1,))
             if s < NS:
                 add_x(s, 1)
                 gate(s, 1)
-            if s >= 1:
-                add_up(s - 1, 1)
-                leave(s - 1)
-            extras(s)
-            if s + 1 < NS:
-                mx(s + 1, 0)
-                mx(s + 1, 1)
+                ct(s)
+            for n in range(1 if s < NS else 2):
+                if todo:
+                    add_up(todo[0][0], (todo[0][1],))
+                    if todo[0][1] == 1:
+                        left.append(todo[0][0])
+                    todo.remove(todo[0])
+            if late:
+                m, c0 = QM[s]
+                w_quant(m, 0, c0, c0 + 256)
+                w_quant(m, 1, c0, c0 + 256)
+                mx(s + 1)
+            if 1 <= s <= NS:
+                times_c(s - 1, 0)
+                times_c(s - 1, 1)
+                if is_last_q(s - 1):
+                    todo.extend([(s - 1, 0), (s - 1, 1)])
+            v_extra(s)
+            t_extra(s)
+            if seen and (s >= NS or len(seen) > 1 or not left):
+                peak(seen[0])
+                seen.remove(seen[0])
 
         pmax = keep.tile([P, 1], F32, name="pmax")
         nc.vector.tensor_reduce(out=pmax[:], in_=stats[:], axis=AX.X, op=ALU.max)
@@ -364,9 +426,13 @@ def tile_childsumtreelstmcell_pa_kernel(tc, x, child_h, child_c, Wf, bWf, Uf, bU
 
         o8a = keep.tile([P, H], FP8, name="o8a")
         o8b = keep.tile([P, H], FP8, name="o8b")
-        nc.vector.tensor_scalar(out=o8a[:], in0=out_sb[:, 0, :], scalar1=fac[:, 0:1], scalar2=None, op0=ALU.mult, saturate=False)
+        VS = 384
         nc.scalar.activation(
-            out=o8b[:], in_=out_sb[:, 1, :], func=ACT.Identity, scale=fac[:, 0:1], bias=zero_col[:, 0:1], saturate=False
+            out=o8b[:, VS:H], in_=out_sb[:, 1, VS:H], func=ACT.Identity, scale=fac[:, 0:1], bias=zero_col[:, 0:1], saturate=False
         )
+        nc.vector.tensor_scalar(out=o8a[:], in0=out_sb[:, 0, :], scalar1=fac[:, 0:1], scalar2=None, op0=ALU.mult, saturate=False)
         nc.sync.dma_start(out=out_1[0:P, :], in_=o8a[:].bitcast(U8))
+        nc.vector.tensor_scalar(
+            out=o8b[:, 0:VS], in0=out_sb[:, 1, 0:VS], scalar1=fac[:, 0:1], scalar2=None, op0=ALU.mult, saturate=False
+        )
         nc.sync.dma_start(out=out_1[P : 2 * P, :], in_=o8b[:].bitcast(U8))

@@ -15,6 +15,8 @@ AX = mybir.AxisListType
 
 P = 128
 NODES, KIDS, D, H = 256, 8, 1024, 1024
+PRE = 15
+XPE = ((5, 1), (7, 1), (9, 1), (11, 1), (13, 1), (15, 1))
 FLOPS = 2 * (NODES + NODES * KIDS) * D * H
 
 
@@ -25,9 +27,9 @@ def tile_childsumtreelstmcell_pa_kernel(tc, x, child_h, child_c, Wf, bWf, Uf, bU
         wst = ctx.enter_context(tc.tile_pool(name="wst", bufs=4))
         hst = ctx.enter_context(tc.tile_pool(name="hst", bufs=3))
         zzp = ctx.enter_context(tc.tile_pool(name="zzp", bufs=3))
-        fpl = ctx.enter_context(tc.tile_pool(name="fpl", bufs=4))
-        ppl = ctx.enter_context(tc.tile_pool(name="ppl", bufs=10))
-        pap = ctx.enter_context(tc.tile_pool(name="pap", bufs=4))
+        fpl = ctx.enter_context(tc.tile_pool(name="fpl", bufs=2))
+        ppl = ctx.enter_context(tc.tile_pool(name="ppl", bufs=5))
+        pap = ctx.enter_context(tc.tile_pool(name="pap", bufs=2))
         ps_z = ctx.enter_context(tc.psum_pool(name="ps_z", bufs=3))
         ps_ct = ctx.enter_context(tc.psum_pool(name="ps_ct", bufs=2))
         ps_tr = ctx.enter_context(tc.psum_pool(name="ps_tr", bufs=3))
@@ -76,8 +78,8 @@ def tile_childsumtreelstmcell_pa_kernel(tc, x, child_h, child_c, Wf, bWf, Uf, bU
         load_h(1, 1)
         load_c(1, 0, 0)
         load_w(0, 1)
-        load_c(1, 1, 0)
         load_w(1, 1)
+        load_c(1, 1, 0)
         load_c(0, 0, 1)
         load_c(0, 1, 1)
         load_c(1, 0, 1)
@@ -194,15 +196,17 @@ def tile_childsumtreelstmcell_pa_kernel(tc, x, child_h, child_c, Wf, bWf, Uf, bU
         steps = [(a, q, jp) for a in (0, 1) for q in (0, 1) for jp in (0, 1)]
         steps += [(a, q, jp) for a in (0, 1) for jp in (2, 3) for q in (0, 1)]
         NS = len(steps)
-        z_t, ct_t, zz_t, f_t, p_t, o_t = {}, {}, {}, {}, {}, {}
+        z_t, ct_t, zz_t, f_t, p_t, o_t, pw_t = {}, {}, {}, {}, {}, {}, {}
 
         def mx(s, bs=(0, 1)):
             a, q, jp = steps[s]
             qc = slice(512 * q, 512 * (q + 1))
+            ac = slice(P * a, P * (a + 1))
             for b in bs:
                 z = ps_z.tile([P, 512], F32, name="z", tag="z")
                 z_t[(s, b)] = z
                 jc = slice(P * (2 * jp + b), P * (2 * jp + b + 1))
+                on_pe = (s, b) in XPE
                 for g in (0, 1):
                     nc.tensor.matmul_mx(
                         out=z[:],
@@ -211,8 +215,20 @@ def tile_childsumtreelstmcell_pa_kernel(tc, x, child_h, child_c, Wf, bWf, Uf, bU
                         rhs=h_codes[:, a, g, qc].bitcast(FP8X4),
                         rhs_scale=h_scales[:, a, g, qc],
                         start=(g == 0),
-                        stop=(g == 1),
+                        stop=(g == 1 and not on_pe),
                     )
+                if on_pe:
+                    for g in (0, 1):
+                        for kk in range(4):
+                            nc.tensor.matmul_mx(
+                                out=z[:, P * kk : P * (kk + 1)],
+                                lhsT=w_codes[:, 0, g, jc].bitcast(FP8X4),
+                                lhsT_scale=w_scales[:, 0, g, jc],
+                                rhs=x_codes[:, g, ac].bitcast(FP8X4),
+                                rhs_scale=x_scales[:, g, ac],
+                                start=False,
+                                stop=(g == 1 and kk == 3),
+                            )
 
         def ct(s):
             a, q, jp = steps[s]
@@ -225,6 +241,8 @@ def tile_childsumtreelstmcell_pa_kernel(tc, x, child_h, child_c, Wf, bWf, Uf, bU
 
         def add_x(s, b):
             a, q, jp = steps[s]
+            if (s, b) in XPE:
+                return
             zz = zzp.tile([P, 512], F32, name="zz", tag="zz")
             zz_t[(s, b)] = zz
             nc.vector.tensor_tensor(
@@ -235,18 +253,25 @@ def tile_childsumtreelstmcell_pa_kernel(tc, x, child_h, child_c, Wf, bWf, Uf, bU
             )
 
         def gate(s, b):
-            f = fpl.tile([P, 512], F32, name="f", tag="f")
-            f_t[(s, b)] = f
-            nc.scalar.activation(out=f[:], in_=zz_t[(s, b)][:], func=ACT.Sigmoid)
+            j = 2 * steps[s][2] + b
+            if b == 0:
+                f_new = fpl.tile([P, 2, 512], F32, name="f", tag="f")
+                f_t[s] = f_new
+            if (s, b) in XPE:
+                nc.scalar.activation(out=f_t[s][:, b, :], in_=z_t[(s, b)][:], func=ACT.Sigmoid, bias=bsum[:, j : j + 1], scale=1.0)
+            else:
+                nc.scalar.activation(out=f_t[s][:, b, :], in_=zz_t[(s, b)][:], func=ACT.Sigmoid)
 
-        def times_c(s, b):
+        def times_c(s):
             a, q, jp = steps[s]
-            p = ppl.tile([P, 512], F32, name="p", tag="p")
-            p_t[(a, q, jp, b)] = p
+            p = ppl.tile([P, 2, 512], F32, name="p", tag="p")
+            pw_t[(a, q, jp)] = p
+            for b in (0, 1):
+                p_t[(a, q, jp, b)] = p[:, b, :]
             nc.vector.tensor_tensor(
                 out=p[:],
-                in0=f_t[(s, b)][:],
-                in1=ct_t[s][:].rearrange("p k n -> p (k n)").bitcast(BF16).rearrange("p (x e) -> p x e", e=2)[:, :, b],
+                in0=f_t[s][:],
+                in1=ct_t[s][:].rearrange("p k n -> p (k n)").bitcast(BF16).rearrange("p (x e) -> p e x", e=2),
                 op=ALU.mult,
             )
 
@@ -273,10 +298,10 @@ def tile_childsumtreelstmcell_pa_kernel(tc, x, child_h, child_c, Wf, bWf, Uf, bU
 
         def pre_add(s):
             a, q, jp = steps[s]
+            t = pap.tile([P, 2, 512], F32, name="pa", tag="pa")
             for b in (0, 1):
-                t = pap.tile([P, 512], F32, name="pa", tag="pa")
-                pa_t[(a, jp, b)] = t
-                nc.gpsimd.tensor_tensor(out=t[:], in0=p_t[(a, 0, jp, b)][:], in1=p_t[(a, 1, jp, b)][:], op=ALU.add)
+                pa_t[(a, jp, b)] = t[:, b, :]
+            nc.gpsimd.tensor_tensor(out=t[:], in0=pw_t[(a, 0, jp)][:], in1=pw_t[(a, 1, jp)][:], op=ALU.add)
 
         n_done = [0]
 
@@ -295,7 +320,7 @@ def tile_childsumtreelstmcell_pa_kernel(tc, x, child_h, child_c, Wf, bWf, Uf, bU
 
         for i in (0, 1):
             h_tr(0, 0, 0, i)
-            h_cp(0, 0, 0, i, "v")
+            h_cp(0, 0, 0, i, "s")
             h_tr(0, 0, 1, i)
             h_cp(0, 0, 1, i, "s")
         h_quant(0, 0, 0)
@@ -332,10 +357,10 @@ def tile_childsumtreelstmcell_pa_kernel(tc, x, child_h, child_c, Wf, bWf, Uf, bU
                 h_cp(0, 1, g, i, "s")
 
         HT = {1: (1, 0), 2: (1, 1)}
-        CP = {5: (0, 512), 6: (0, 768), 7: (1, 512), 8: (1, 768)}
-        QU = {6: (0, 512), 7: (0, 768), 8: (1, 768)}
-        QM = {7: (1, 512)}
-        XF = {6: 2, 7: 3}
+        CP = {4: (0, 512), 5: (1, 512), 6: (0, 768), 7: (1, 768)}
+        QU = {5: (0, 512), 6: (1, 512), 7: (0, 768), 8: (1, 768)}
+        QM = {}
+        XF = {5: 2, 7: 3}
 
         def t_extra(s):
             if s in HT:
@@ -403,9 +428,10 @@ def tile_childsumtreelstmcell_pa_kernel(tc, x, child_h, child_c, Wf, bWf, Uf, bU
                 w_quant(m, 1, c0, c0 + 256)
                 mx(s + 1)
             if 1 <= s <= NS:
-                times_c(s - 1, 0)
-                times_c(s - 1, 1)
+                times_c(s - 1)
                 if is_last_q(s - 1):
+                    if s - 1 < PRE:
+                        pre_add(s - 1)
                     todo.extend([(s - 1, 0), (s - 1, 1)])
             v_extra(s)
             t_extra(s)

@@ -33,7 +33,6 @@ def tile_childsumtreelstmcell_pa_kernel(tc, x, child_h, child_c, Wf, bWf, Uf, bU
         ps_z = ctx.enter_context(tc.psum_pool(name="ps_z", bufs=3))
         ps_ct = ctx.enter_context(tc.psum_pool(name="ps_ct", bufs=2))
         ps_tr = ctx.enter_context(tc.psum_pool(name="ps_tr", bufs=3))
-        ctx.enter_context(tc.manual_schedule())
 
         ident_f = keep.tile([P, P], F32, name="ident_f")
         make_identity(nc, ident_f[:])

@@ -15,8 +15,8 @@ AX = mybir.AxisListType
 
 P = 128
 NODES, KIDS, D, H = 256, 8, 1024, 1024
-PRE = 15
-XPE = ((5, 1), (7, 1), (9, 1), (11, 1), (13, 1), (15, 1))
+PRE = 0
+XPE = ()
 FLOPS = 2 * (NODES + NODES * KIDS) * D * H
 
 
@@ -33,6 +33,7 @@ def tile_childsumtreelstmcell_pa_kernel(tc, x, child_h, child_c, Wf, bWf, Uf, bU
         ps_z = ctx.enter_context(tc.psum_pool(name="ps_z", bufs=3))
         ps_ct = ctx.enter_context(tc.psum_pool(name="ps_ct", bufs=2))
         ps_tr = ctx.enter_context(tc.psum_pool(name="ps_tr", bufs=3))
+        ctx.enter_context(tc.manual_schedule())
 
         ident_f = keep.tile([P, P], F32, name="ident_f")
         make_identity(nc, ident_f[:])

@@ -356,7 +356,7 @@ def tile_childsumtreelstmcell_pa_kernel(tc, x, child_h, child_c, Wf, bWf, Uf, bU
                 h_tr(0, 1, g, i)
                 h_cp(0, 1, g, i, "s")
 
-        HT = {1: (1, 0), 2: (1, 1)}
+        HT = {0: (1, 0, 0), 1: (1, 0, 1), 2: (1, 1, 0), 3: (1, 1, 1)}
         CP = {4: (0, 512), 5: (1, 512), 6: (0, 768), 7: (1, 768)}
         QU = {5: (0, 512), 6: (1, 512), 7: (0, 768), 8: (1, 768)}
         QM = {}
@@ -364,11 +364,10 @@ def tile_childsumtreelstmcell_pa_kernel(tc, x, child_h, child_c, Wf, bWf, Uf, bU
 
         def t_extra(s):
             if s in HT:
-                a, q = HT[s]
-                for g in (0, 1):
-                    for i in (0, 1):
-                        h_tr(a, q, g, i)
-                        h_cp(a, q, g, i, "s")
+                a, q, g = HT[s]
+                for i in (0, 1):
+                    h_tr(a, q, g, i)
+                    h_cp(a, q, g, i, "s")
             if s in XF:
                 xf_mm(XF[s])
                 xf_ev(XF[s])
@@ -384,9 +383,8 @@ def tile_childsumtreelstmcell_pa_kernel(tc, x, child_h, child_c, Wf, bWf, Uf, bU
                 h_quant(0, 1, 0)
                 h_quant(0, 1, 1)
             if s - 1 in HT:
-                a, q = HT[s - 1]
-                h_quant(a, q, 0)
-                h_quant(a, q, 1)
+                a, q, g = HT[s - 1]
+                h_quant(a, q, g)
             if s in QU:
                 m, c0 = QU[s]
                 w_quant(m, 0, c0, c0 + 256)

@@ -106,7 +106,7 @@ def tile_childsumtreelstmcell_pa_kernel(tc, x, child_h, child_c, Wf, bWf, Uf, bU
                 nc.gpsimd.tensor_scalar(out=out, in0=in_, scalar1=1.0, scalar2=0.0, op0=ALU.mult, op1=ALU.add)
 
         def bias():
-            bps = ps_tr.tile([P, P], F32, name="bps", tag="tr")
+            bps = ps_ct.tile([P, P], F32, name="bps", tag="ct")
             nc.tensor.transpose(bps[:], brow[:].bitcast(F32), ident_f[:])
             nc.vector.tensor_copy(out=bcol[:], in_=bps[:, 0:8].bitcast(BF16))
             nc.vector.tensor_tensor(out=bsum[:], in0=bcol[:, 0:8], in1=bcol[:, 8:16], op=ALU.add)
@@ -117,9 +117,9 @@ def tile_childsumtreelstmcell_pa_kernel(tc, x, child_h, child_c, Wf, bWf, Uf, bU
 
         hgrp, htr = {}, {}
 
-        def h_tr(a, q, g, i):
+        def h_tr(a, q, g, i, pool=ps_tr, tag="tr"):
             words = h_sb[(a, q, i)][:].rearrange("p k d -> p (k d)").bitcast(F32)
-            tr = ps_tr.tile([P, 2, 2, P], F32, name="tr", tag="tr")
+            tr = pool.tile([P, 2, 2, P], F32, name="tr", tag=tag)
             htr[(a, q, g, i)] = tr
             for kk in (0, 1):
                 turn(words, 512 * kk, g, tr[:, kk, :, :])
@@ -139,11 +139,11 @@ def tile_childsumtreelstmcell_pa_kernel(tc, x, child_h, child_c, Wf, bWf, Uf, bU
 
         xgrp = {}
 
-        def x_turn(g, eng):
+        def x_turn(g, eng, pool=ps_tr, tag="tr"):
             words = x_sb[:].rearrange("p a d -> p (a d)").bitcast(F32)
             grp = hst.tile([P, NODES * 4], BF16, name="xgrp", tag="xgrp", align_bytes=64)
             xgrp[g] = grp
-            tr = ps_tr.tile([P, 2, 2, P], F32, name="tr", tag="tr")
+            tr = pool.tile([P, 2, 2, P], F32, name="tr", tag=tag)
             for a in (0, 1):
                 turn(words, 512 * a, g, tr[:, a, :, :])
             copy_on(eng, grp[:].bitcast(F32).rearrange("p (a n u) -> p a n u", a=2, u=2), tr[:].rearrange("p a u n -> p a n u"))
@@ -321,12 +321,11 @@ def tile_childsumtreelstmcell_pa_kernel(tc, x, child_h, child_c, Wf, bWf, Uf, bU
         for i in (0, 1):
             h_tr(0, 0, 0, i)
             h_cp(0, 0, 0, i, "s")
-            h_tr(0, 0, 1, i)
+            h_tr(0, 0, 1, i, ps_z, "z")
             h_cp(0, 0, 1, i, "s")
         h_quant(0, 0, 0)
         x_turn(0, "s")
-        x_turn(1, "s")
-        bias()
+        x_turn(1, "s", ps_z, "z")
         h_quant(0, 0, 1)
         w_copy(0, 0, 0, 256, "v")
         w_copy(0, 0, 256, 512, "s")
@@ -337,6 +336,7 @@ def tile_childsumtreelstmcell_pa_kernel(tc, x, child_h, child_c, Wf, bWf, Uf, bU
         w_copy(0, 1, 256, 512, "s")
         w_quant(0, 0, 256, 512)
         w_quant(0, 1, 0, 256)
+        bias()
         xf_mm(0)
         w_copy(1, 0, 0, 256, "v")
         w_copy(1, 0, 256, 512, "s")
@@ -348,13 +348,15 @@ def tile_childsumtreelstmcell_pa_kernel(tc, x, child_h, child_c, Wf, bWf, Uf, bU
         w_copy(1, 1, 256, 512, "s")
         w_quant(1, 0, 256, 512)
         w_quant(1, 1, 0, 256)
+        for i in (0, 1):
+            h_tr(0, 1, 0, i, ps_ct, "ct")
+            h_cp(0, 1, 0, i, "s")
         mx(0)
         xf_ev(1)
         w_quant(1, 1, 256, 512)
-        for g in (0, 1):
-            for i in (0, 1):
-                h_tr(0, 1, g, i)
-                h_cp(0, 1, g, i, "s")
+        for i in (0, 1):
+            h_tr(0, 1, 1, i)
+            h_cp(0, 1, 1, i, "s")
 
         HT = {0: (1, 0, 0), 1: (1, 0, 1), 2: (1, 1, 0), 3: (1, 1, 1)}
         CP = {4: (0, 512), 5: (1, 512), 6: (0, 768), 7: (1, 768)}

@@ -268,12 +268,12 @@ def tile_childsumtreelstmcell_pa_kernel(tc, x, child_h, child_c, Wf, bWf, Uf, bU
             pw_t[(a, q, jp)] = p
             for b in (0, 1):
                 p_t[(a, q, jp, b)] = p[:, b, :]
-            nc.vector.tensor_tensor(
-                out=p[:],
-                in0=f_t[s][:],
-                in1=ct_t[s][:].rearrange("p k n -> p (k n)").bitcast(BF16).rearrange("p (x e) -> p e x", e=2),
-                op=ALU.mult,
-            )
+            c_view = ct_t[s][:].rearrange("p k n -> p (k n)").bitcast(BF16).rearrange("p (x e) -> p e x", e=2)
+            if s == NS - 1:
+                for b in (0, 1):
+                    nc.vector.tensor_tensor(out=p[:, b, :], in0=f_t[s][:, b, :], in1=c_view[:, b, :], op=ALU.mult)
+            else:
+                nc.vector.tensor_tensor(out=p[:], in0=f_t[s][:], in1=c_view, op=ALU.mult)
 
         def add_up(s, bs=(0, 1)):
             a, q, jp = steps[s]
@@ -406,7 +406,6 @@ def tile_childsumtreelstmcell_pa_kernel(tc, x, child_h, child_c, Wf, bWf, Uf, bU
                 leave(left[0])
                 seen.append(left[0])
                 left.remove(left[0])
-            s_extra(s)
             if s < NS:
                 add_x(s, 0)
                 gate(s, 0)
@@ -416,6 +415,7 @@ def tile_childsumtreelstmcell_pa_kernel(tc, x, child_h, child_c, Wf, bWf, Uf, bU
                 add_x(s, 1)
                 gate(s, 1)
                 ct(s)
+            s_extra(s)
             for n in range(1 if s < NS else 2):
                 if todo:
                     add_up(todo[0][0], (todo[0][1],))

@@ -16,7 +16,7 @@ AX = mybir.AxisListType
 P = 128
 NODES, KIDS, D, H = 256, 8, 1024, 1024
 PRE = 0
-XPE = ()
+XPE = ((4, 1), (6, 1))
 FLOPS = 2 * (NODES + NODES * KIDS) * D * H
 
 

@@ -17,6 +17,8 @@ P = 128
 NODES, KIDS, D, H = 256, 8, 1024, 1024
 PRE = 0
 XPE = ((4, 1), (6, 1))
+GS = (10, 12)
+PS = ()
 FLOPS = 2 * (NODES + NODES * KIDS) * D * H
 
 
@@ -27,7 +29,8 @@ def tile_childsumtreelstmcell_pa_kernel(tc, x, child_h, child_c, Wf, bWf, Uf, bU
         wst = ctx.enter_context(tc.tile_pool(name="wst", bufs=4))
         hst = ctx.enter_context(tc.tile_pool(name="hst", bufs=3))
         zzp = ctx.enter_context(tc.tile_pool(name="zzp", bufs=3))
-        fpl = ctx.enter_context(tc.tile_pool(name="fpl", bufs=2))
+        fpl = ctx.enter_context(tc.tile_pool(name="fpl", bufs=3))
+        ctp = ctx.enter_context(tc.tile_pool(name="ctp", bufs=2))
         ppl = ctx.enter_context(tc.tile_pool(name="ppl", bufs=5))
         pap = ctx.enter_context(tc.tile_pool(name="pap", bufs=2))
         ps_z = ctx.enter_context(tc.psum_pool(name="ps_z", bufs=3))
@@ -275,6 +278,26 @@ def tile_childsumtreelstmcell_pa_kernel(tc, x, child_h, child_c, Wf, bWf, Uf, bU
             else:
                 nc.vector.tensor_tensor(out=p[:], in0=f_t[s][:], in1=c_view, op=ALU.mult)
 
+        cts_t = {}
+
+        def ct_out(s):
+            t = ctp.tile([P, 512], F32, name="cts", tag="cts")
+            cts_t[s] = t
+            nc.scalar.copy(out=t[:], in_=ct_t[s][:].rearrange("p k n -> p (k n)"))
+
+        def times_c_g(s):
+            a, q, jp = steps[s]
+            p = ppl.tile([P, 2, 512], F32, name="p", tag="p")
+            pw_t[(a, q, jp)] = p
+            for b in (0, 1):
+                p_t[(a, q, jp, b)] = p[:, b, :]
+            nc.gpsimd.tensor_tensor(
+                out=p[:],
+                in0=f_t[s][:],
+                in1=cts_t[s][:].bitcast(BF16).rearrange("p (x e) -> p e x", e=2),
+                op=ALU.mult,
+            )
+
         def add_up(s, bs=(0, 1)):
             a, q, jp = steps[s]
             if 0 in bs:
@@ -415,6 +438,9 @@ def tile_childsumtreelstmcell_pa_kernel(tc, x, child_h, child_c, Wf, bWf, Uf, bU
                 add_x(s, 1)
                 gate(s, 1)
                 ct(s)
+                if s in GS:
+                    ct_out(s)
+                    times_c_g(s)
             s_extra(s)
             for n in range(1 if s < NS else 2):
                 if todo:
@@ -428,9 +454,10 @@ def tile_childsumtreelstmcell_pa_kernel(tc, x, child_h, child_c, Wf, bWf, Uf, bU
                 w_quant(m, 1, c0, c0 + 256)
                 mx(s + 1)
             if 1 <= s <= NS:
-                times_c(s - 1)
+                if s - 1 not in GS:
+                    times_c(s - 1)
                 if is_last_q(s - 1):
-                    if s - 1 < PRE:
+                    if s - 1 in PS:
                         pre_add(s - 1)
                     todo.extend([(s - 1, 0), (s - 1, 1)])
             v_extra(s)

@@ -95,8 +95,7 @@ def tile_childsumtreelstmcell_pa_kernel(tc, x, child_h, child_c, Wf, bWf, Uf, bU
         x_codes = keep.tile([P, 2, NODES], U32, name="x_codes", align_bytes=64)
         x_scales = keep.tile([P, 2, NODES], U8, name="x_scales", align_bytes=64)
         xfT = keep.tile([P, 8, NODES], F32, name="xfT")
-        out_sb = keep.tile([P, 2, H], F32, name="out_sb")
-        stats = keep.tile([P, 8], F32, name="stats")
+        out_sb = keep.tile([P, 2 * H + 8], F32, name="out_sb")
         bcol = keep.tile([P, 16], F32, name="bcol")
         bsum = keep.tile([P, 8], F32, name="bsum")
 
@@ -327,19 +326,27 @@ def tile_childsumtreelstmcell_pa_kernel(tc, x, child_h, child_c, Wf, bWf, Uf, bU
             nc.gpsimd.tensor_tensor(out=t[:], in0=pw_t[(a, 0, jp)][:], in1=pw_t[(a, 1, jp)][:], op=ALU.add)
 
         n_done = [0]
+        pmax = keep.tile([P, 1], F32, name="pmax")
 
         def leave(s):
             a, q, jp = steps[s]
             cols = slice(256 * jp, 256 * (jp + 1))
-            nc.scalar.copy(out=out_sb[:, a, cols].rearrange("p (m b) -> p m b", b=2), in_=o_t[s][:].rearrange("p b m -> p m b"))
-            nc.sync.dma_start(out=out_0[P * a : P * (a + 1), cols], in_=out_sb[:, a, cols])
+            here = slice(H * a + 256 * jp, H * a + 256 * (jp + 1))
+            nc.scalar.copy(out=out_sb[:, here].rearrange("p (m b) -> p m b", b=2), in_=o_t[s][:].rearrange("p b m -> p m b"))
+            nc.sync.dma_start(out=out_0[P * a : P * (a + 1), cols], in_=out_sb[:, here])
 
         def peak(s):
             a, q, jp = steps[s]
-            cols = slice(256 * jp, 256 * (jp + 1))
+            c0 = H * a + 256 * jp
             i = n_done[0]
             n_done[0] = i + 1
-            nc.vector.tensor_reduce(out=stats[:, i : i + 1], in_=out_sb[:, a, cols], axis=AX.X, op=ALU.max, apply_absolute_value=True)
+            if i < 7:
+                nc.vector.tensor_reduce(
+                    out=out_sb[:, 2 * H + i : 2 * H + i + 1], in_=out_sb[:, c0 : c0 + 256], axis=AX.X, op=ALU.max, apply_absolute_value=True
+                )
+            else:
+                assert c0 + 256 == 2 * H
+                nc.vector.tensor_reduce(out=pmax[:], in_=out_sb[:, c0 : 2 * H + 7], axis=AX.X, op=ALU.max, apply_absolute_value=True)
 
         for i in (0, 1):
             h_tr(0, 0, 0, i)
@@ -466,26 +473,23 @@ def tile_childsumtreelstmcell_pa_kernel(tc, x, child_h, child_c, Wf, bWf, Uf, bU
                 peak(seen[0])
                 seen.remove(seen[0])
 
-        pmax = keep.tile([P, 1], F32, name="pmax")
-        nc.vector.tensor_reduce(out=pmax[:], in_=stats[:], axis=AX.X, op=ALU.max)
         aps = ps_tr.tile([P, P], F32, name="aps", tag="tr")
         nc.tensor.transpose(aps[:], pmax[:, 0:1].to_broadcast([P, P]), ident_f[:])
-        amax = keep.tile([P, 1], F32, name="amax")
-        nc.vector.tensor_reduce(out=amax[:], in_=aps[:], axis=AX.X, op=ALU.max)
-        rec = keep.tile([P, 1], F32, name="rec")
-        nc.vector.reciprocal(out=rec[:], in_=amax[:])
+        scaled = keep.tile([P, P], F32, name="scaled")
+        scl = keep.tile([P, 1], F32, name="scl")
+        nc.vector.tensor_scalar(out=scaled[:], in0=aps[:], scalar1=1.0 / 448.0, scalar2=None, op0=ALU.mult, op1=ALU.max, accum_out=scl[:])
         fac = keep.tile([P, 1], F32, name="fac")
-        nc.vector.tensor_scalar(out=fac[:], in0=rec[:], scalar1=448.0, scalar2=None, op0=ALU.mult)
+        nc.vector.reciprocal(out=fac[:], in_=scl[:])
 
         o8a = keep.tile([P, H], FP8, name="o8a")
         o8b = keep.tile([P, H], FP8, name="o8b")
         VS = 384
         nc.scalar.activation(
-            out=o8b[:, VS:H], in_=out_sb[:, 1, VS:H], func=ACT.Identity, scale=fac[:, 0:1], bias=zero_col[:, 0:1], saturate=False
+            out=o8b[:, VS:H], in_=out_sb[:, H + VS : 2 * H], func=ACT.Identity, scale=fac[:, 0:1], bias=zero_col[:, 0:1], saturate=False
         )
-        nc.vector.tensor_scalar(out=o8a[:], in0=out_sb[:, 0, :], scalar1=fac[:, 0:1], scalar2=None, op0=ALU.mult, saturate=False)
+        nc.vector.tensor_scalar(out=o8a[:], in0=out_sb[:, 0:H], scalar1=fac[:, 0:1], scalar2=None, op0=ALU.mult, saturate=False)
         nc.sync.dma_start(out=out_1[0:P, :], in_=o8a[:].bitcast(U8))
         nc.vector.tensor_scalar(
-            out=o8b[:, 0:VS], in0=out_sb[:, 1, 0:VS], scalar1=fac[:, 0:1], scalar2=None, op0=ALU.mult, saturate=False
+            out=o8b[:, 0:VS], in0=out_sb[:, H : H + VS], scalar1=fac[:, 0:1], scalar2=None, op0=ALU.mult, saturate=False
         )
         nc.sync.dma_start(out=out_1[P : 2 * P, :], in_=o8b[:].bitcast(U8))

@@ -44,6 +44,15 @@ def tile_childsumtreelstmcell_pa_kernel(tc, x, child_h, child_c, Wf, bWf, Uf, bU
         nc.vector.memset(zero_col[:], 0.0)
         warm = keep.tile([P, 1], F32, name="warm")
         nc.scalar.activation(out=warm[:], in_=zero_col[:], func=ACT.Sigmoid)
+        dz = keep.tile([P, 512], BF16, name="dz")
+        nc.vector.memset(dz[:], 0.0)
+
+        def warm_pe(n):
+            if n:
+                t = ps_ct.tile([P, 512], F32, name="idle", tag="ct")
+                for r in range(n):
+                    nc.tensor.matmul(out=t[:], lhsT=dz[:, 0:P], rhs=dz[:], start=True, stop=True)
+
         brow = keep.tile([P, 2 * P], BF16, name="brow")
         nc.vector.memset(brow[:], 0.0)
         nc.scalar.dma_start(out=brow[0:4, :], in_=bWf.rearrange("(r c) -> r c", c=2 * P))
@@ -174,7 +183,7 @@ def tile_childsumtreelstmcell_pa_kernel(tc, x, child_h, child_c, Wf, bWf, Uf, bU
 
         xps = {}
 
-        def xf_mm(sc):
+        def xf_mm(sc, fill=0):
             ps = ps_tr.tile([P, 2, NODES], F32, name="xps", tag="tr")
             xps[sc] = ps
             for jj in (0, 1):
@@ -189,6 +198,8 @@ def tile_childsumtreelstmcell_pa_kernel(tc, x, child_h, child_c, Wf, bWf, Uf, bU
                         start=(g == 0),
                         stop=(g == 1),
                     )
+                    if jj == 0 and g == 0:
+                        warm_pe(fill)
 
         def xf_ev(sc):
             for jj in (0, 1):
@@ -348,14 +359,17 @@ def tile_childsumtreelstmcell_pa_kernel(tc, x, child_h, child_c, Wf, bWf, Uf, bU
                 assert c0 + 256 == 2 * H
                 nc.vector.tensor_reduce(out=pmax[:], in_=out_sb[:, c0 : 2 * H + 7], axis=AX.X, op=ALU.max, apply_absolute_value=True)
 
+        warm_pe(6)
         for i in (0, 1):
             h_tr(0, 0, 0, i)
             h_cp(0, 0, 0, i, "s")
             h_tr(0, 0, 1, i, ps_z, "z")
             h_cp(0, 0, 1, i, "s")
         h_quant(0, 0, 0)
+        warm_pe(2)
         x_turn(0, "s")
         x_turn(1, "s", ps_z, "z")
+        warm_pe(4)
         h_quant(0, 0, 1)
         w_copy(0, 0, 0, 256, "v")
         w_copy(0, 0, 256, 512, "s")
@@ -367,11 +381,11 @@ def tile_childsumtreelstmcell_pa_kernel(tc, x, child_h, child_c, Wf, bWf, Uf, bU
         w_quant(0, 0, 256, 512)
         w_quant(0, 1, 0, 256)
         bias()
-        xf_mm(0)
+        xf_mm(0, 4)
         w_copy(1, 0, 0, 256, "v")
         w_copy(1, 0, 256, 512, "s")
         w_quant(0, 1, 256, 512)
-        xf_mm(1)
+        xf_mm(1, 2)
         w_quant(1, 0, 0, 256)
         xf_ev(0)
         w_copy(1, 1, 0, 256, "v")
@@ -381,6 +395,7 @@ def tile_childsumtreelstmcell_pa_kernel(tc, x, child_h, child_c, Wf, bWf, Uf, bU
         for i in (0, 1):
             h_tr(0, 1, 0, i, ps_ct, "ct")
             h_cp(0, 1, 0, i, "s")
+        warm_pe(0)
         mx(0)
         xf_ev(1)
         w_quant(1, 1, 256, 512)

@@ -366,10 +366,9 @@ def tile_childsumtreelstmcell_pa_kernel(tc, x, child_h, child_c, Wf, bWf, Uf, bU
             h_tr(0, 0, 1, i, ps_z, "z")
             h_cp(0, 0, 1, i, "s")
         h_quant(0, 0, 0)
-        warm_pe(2)
         x_turn(0, "s")
         x_turn(1, "s", ps_z, "z")
-        warm_pe(4)
+        warm_pe(0)
         h_quant(0, 0, 1)
         w_copy(0, 0, 0, 256, "v")
         w_copy(0, 0, 256, 512, "s")
@@ -381,11 +380,11 @@ def tile_childsumtreelstmcell_pa_kernel(tc, x, child_h, child_c, Wf, bWf, Uf, bU
         w_quant(0, 0, 256, 512)
         w_quant(0, 1, 0, 256)
         bias()
-        xf_mm(0, 4)
+        xf_mm(0, 0)
         w_copy(1, 0, 0, 256, "v")
         w_copy(1, 0, 256, 512, "s")
         w_quant(0, 1, 256, 512)
-        xf_mm(1, 2)
+        xf_mm(1, 0)
         w_quant(1, 0, 0, 256)
         xf_ev(0)
         w_copy(1, 1, 0, 256, "v")

@@ -391,16 +391,17 @@ def tile_childsumtreelstmcell_pa_kernel(tc, x, child_h, child_c, Wf, bWf, Uf, bU
         w_copy(1, 1, 256, 512, "s")
         w_quant(1, 0, 256, 512)
         w_quant(1, 1, 0, 256)
-        for i in (0, 1):
-            h_tr(0, 1, 0, i, ps_ct, "ct")
-            h_cp(0, 1, 0, i, "s")
-        warm_pe(0)
+        h_tr(0, 1, 0, 0, ps_ct, "ct")
+        h_cp(0, 1, 0, 0, "s")
+        h_tr(0, 1, 1, 0)
+        h_cp(0, 1, 1, 0, "s")
         mx(0)
         xf_ev(1)
         w_quant(1, 1, 256, 512)
-        for i in (0, 1):
-            h_tr(0, 1, 1, i)
-            h_cp(0, 1, 1, i, "s")
+        h_tr(0, 1, 0, 1, ps_ct, "ct")
+        h_cp(0, 1, 0, 1, "s")
+        h_tr(0, 1, 1, 1)
+        h_cp(0, 1, 1, 1, "s")
 
         HT = {0: (1, 0, 0), 1: (1, 0, 1), 2: (1, 1, 0), 3: (1, 1, 1)}
         CP = {4: (0, 512), 5: (1, 512), 6: (0, 768), 7: (1, 768)}

@@ -148,6 +148,12 @@ def tile_childsumtreelstmcell_pa_kernel(tc, x, child_h, child_c, Wf, bWf, Uf, bU
                 out=h_codes[:, a, g, cols].bitcast(FP8X4), scales=h_scales[:, a, g, cols], in_=hgrp[(a, q, g)][:]
             )
 
+        def h_quant_half(a, q, g, i):
+            cols = slice(512 * q + 256 * i, 512 * q + 256 * (i + 1))
+            nc.vector.quantize_mx(
+                out=h_codes[:, a, g, cols].bitcast(FP8X4), scales=h_scales[:, a, g, cols], in_=hgrp[(a, q, g)][:, 1024 * i : 1024 * (i + 1)]
+            )
+
         xgrp = {}
 
         def x_turn(g, eng, pool=ps_tr, tag="tr"):
@@ -398,6 +404,8 @@ def tile_childsumtreelstmcell_pa_kernel(tc, x, child_h, child_c, Wf, bWf, Uf, bU
         mx(0)
         xf_ev(1)
         w_quant(1, 1, 256, 512)
+        h_quant_half(0, 1, 0, 0)
+        h_quant_half(0, 1, 1, 0)
         h_tr(0, 1, 0, 1, ps_ct, "ct")
         h_cp(0, 1, 0, 1, "s")
         h_tr(0, 1, 1, 1)
@@ -427,8 +435,8 @@ def tile_childsumtreelstmcell_pa_kernel(tc, x, child_h, child_c, Wf, bWf, Uf, bU
 
         def v_extra(s):
             if s == 0:
-                h_quant(0, 1, 0)
-                h_quant(0, 1, 1)
+                h_quant_half(0, 1, 0, 1)
+                h_quant_half(0, 1, 1, 1)
             if s - 1 in HT:
                 a, q, g = HT[s - 1]
                 h_quant(a, q, g)

from contextlib import ExitStack

import concourse.mybir as mybir
from concourse.masks import make_identity

F32 = mybir.dt.float32
BF16 = mybir.dt.bfloat16
U32 = mybir.dt.uint32
U8 = mybir.dt.uint8
FP8 = mybir.dt.float8_e4m3fn
FP8X4 = mybir.dt.float8_e4m3fn_x4
ACT = mybir.ActivationFunctionType
ALU = mybir.AluOpType
AX = mybir.AxisListType

P = 128
NODES, KIDS, D, H = 256, 8, 1024, 1024
PRE = 0
XPE = ((4, 1), (6, 1))
GS = (10, 12)
PS = ()
FLOPS = 2 * (NODES + NODES * KIDS) * D * H


def tile_childsumtreelstmcell_pa_kernel(tc, x, child_h, child_c, Wf, bWf, Uf, bUf, out_0, out_1):
    nc = tc.nc
    with ExitStack() as ctx:
        keep = ctx.enter_context(tc.tile_pool(name="keep", bufs=1))
        wst = ctx.enter_context(tc.tile_pool(name="wst", bufs=4))
        hst = ctx.enter_context(tc.tile_pool(name="hst", bufs=3))
        zzp = ctx.enter_context(tc.tile_pool(name="zzp", bufs=3))
        fpl = ctx.enter_context(tc.tile_pool(name="fpl", bufs=3))
        ctp = ctx.enter_context(tc.tile_pool(name="ctp", bufs=2))
        ppl = ctx.enter_context(tc.tile_pool(name="ppl", bufs=5))
        pap = ctx.enter_context(tc.tile_pool(name="pap", bufs=2))
        ps_z = ctx.enter_context(tc.psum_pool(name="ps_z", bufs=3))
        ps_ct = ctx.enter_context(tc.psum_pool(name="ps_ct", bufs=2))
        ps_tr = ctx.enter_context(tc.psum_pool(name="ps_tr", bufs=3))
        ctx.enter_context(tc.manual_schedule())

        ident_f = keep.tile([P, P], F32, name="ident_f")
        make_identity(nc, ident_f[:])
        zero_col = keep.tile([P, 1], F32, name="zero_col")
        nc.vector.memset(zero_col[:], 0.0)
        warm = keep.tile([P, 1], F32, name="warm")
        nc.scalar.activation(out=warm[:], in_=zero_col[:], func=ACT.Sigmoid)
        dz = keep.tile([P, 512], BF16, name="dz")
        nc.vector.memset(dz[:], 0.0)

        def warm_pe(n):
            if n:
                t = ps_ct.tile([P, 512], F32, name="idle", tag="ct")
                for r in range(n):
                    nc.tensor.matmul(out=t[:], lhsT=dz[:, 0:P], rhs=dz[:], start=True, stop=True)

        brow = keep.tile([P, 2 * P], BF16, name="brow")
        nc.vector.memset(brow[:], 0.0)
        nc.scalar.dma_start(out=brow[0:4, :], in_=bWf.rearrange("(r c) -> r c", c=2 * P))
        nc.scalar.dma_start(out=brow[4:8, :], in_=bUf.rearrange("(r c) -> r c", c=2 * P))

        def load(name, shape, src):
            t = keep.tile(shape, BF16, name=name)
            nc.sync.dma_start(out=t[:], in_=src)
            return t

        wraw, h_sb, c_sb = {}, {}, {}

        def load_w(m, hh):
            for g in (0, 1):
                src = (Wf, Uf)[m][512 * g : 512 * (g + 1), 512 * hh : 512 * (hh + 1)].rearrange("(p t) w -> p t w", t=4)
                wraw[(m, g, hh)] = load("wraw%d_%d_%d" % (m, g, hh), [P, 4, 512], src)

        def load_h(a, q):
            for i in (0, 1):
                k0 = 4 * q + 2 * i
                h_sb[(a, q, i)] = load("h%d_%d_%d" % (a, q, i), [P, 2, D], child_h[P * a : P * (a + 1), k0 : k0 + 2, :])

        def load_c(a, q, hh):
            src = child_c[P * a : P * (a + 1), 4 * q : 4 * q + 4, 512 * hh : 512 * (hh + 1)]
            c_sb[(a, q, hh)] = load("c%d_%d_%d" % (a, q, hh), [P, 4, 512], src)

        load_h(0, 0)
        x_sb = load("x_sb", [P, 2, D], x.rearrange("(a p) d -> p a d", p=P))
        load_w(0, 0)
        load_w(1, 0)
        load_h(0, 1)
        load_c(0, 0, 0)
        load_h(1, 0)
        load_c(0, 1, 0)
        load_h(1, 1)
        load_c(1, 0, 0)
        load_w(0, 1)
        load_w(1, 1)
        load_c(1, 1, 0)
        load_c(0, 0, 1)
        load_c(0, 1, 1)
        load_c(1, 0, 1)
        load_c(1, 1, 1)

        w_codes = keep.tile([P, 2, 2, H], U32, name="w_codes", align_bytes=64)
        w_scales = keep.tile([P, 2, 2, H], U8, name="w_scales", align_bytes=64)
        h_codes = keep.tile([P, 2, 2, KIDS * P], U32, name="h_codes", align_bytes=64)
        h_scales = keep.tile([P, 2, 2, KIDS * P], U8, name="h_scales", align_bytes=64)
        x_codes = keep.tile([P, 2, NODES], U32, name="x_codes", align_bytes=64)
        x_scales = keep.tile([P, 2, NODES], U8, name="x_scales", align_bytes=64)
        xfT = keep.tile([P, 8, NODES], F32, name="xfT")
        out_sb = keep.tile([P, 2 * H + 8], F32, name="out_sb")
        bcol = keep.tile([P, 16], F32, name="bcol")
        bsum = keep.tile([P, 8], F32, name="bsum")

        def copy_on(eng, out, in_):
            if eng == "v":
                nc.vector.tensor_copy(out=out, in_=in_)
            elif eng == "s":
                nc.scalar.copy(out=out, in_=in_)
            else:
                nc.gpsimd.tensor_scalar(out=out, in0=in_, scalar1=1.0, scalar2=0.0, op0=ALU.mult, op1=ALU.add)

        def bias():
            bps = ps_ct.tile([P, P], F32, name="bps", tag="ct")
            nc.tensor.transpose(bps[:], brow[:].bitcast(F32), ident_f[:])
            nc.vector.tensor_copy(out=bcol[:], in_=bps[:, 0:8].bitcast(BF16))
            nc.vector.tensor_tensor(out=bsum[:], in0=bcol[:, 0:8], in1=bcol[:, 8:16], op=ALU.add)

        def turn(words, base, g, dst):
            for u in (0, 1):
                nc.tensor.transpose(dst[:, u, :], words[:, base + 256 * g + u : base + 256 * (g + 1) : 2], ident_f[:])

        hgrp, htr = {}, {}

        def h_tr(a, q, g, i, pool=ps_tr, tag="tr"):
            words = h_sb[(a, q, i)][:].rearrange("p k d -> p (k d)").bitcast(F32)
            tr = pool.tile([P, 2, 2, P], F32, name="tr", tag=tag)
            htr[(a, q, g, i)] = tr
            for kk in (0, 1):
                turn(words, 512 * kk, g, tr[:, kk, :, :])

        def h_cp(a, q, g, i, eng):
            if i == 0:
                grp = hst.tile([P, 4 * P * 4], BF16, name="hgrp", tag="hgrp", align_bytes=64)
                hgrp[(a, q, g)] = grp
            gw = hgrp[(a, q, g)][:].bitcast(F32).rearrange("p (k n u) -> p k n u", k=4, u=2)
            copy_on(eng, gw[:, 2 * i : 2 * i + 2, :, :], htr[(a, q, g, i)][:].rearrange("p i u n -> p i n u"))

        def h_quant(a, q, g):
            cols = slice(512 * q, 512 * (q + 1))
            nc.vector.quantize_mx(
                out=h_codes[:, a, g, cols].bitcast(FP8X4), scales=h_scales[:, a, g, cols], in_=hgrp[(a, q, g)][:]
            )

        def h_quant_half(a, q, g, i):
            cols = slice(512 * q + 256 * i, 512 * q + 256 * (i + 1))
            nc.vector.quantize_mx(
                out=h_codes[:, a, g, cols].bitcast(FP8X4), scales=h_scales[:, a, g, cols], in_=hgrp[(a, q, g)][:, 1024 * i : 1024 * (i + 1)]
            )

        xgrp = {}

        def x_turn(g, eng, pool=ps_tr, tag="tr"):
            words = x_sb[:].rearrange("p a d -> p (a d)").bitcast(F32)
            grp = hst.tile([P, NODES * 4], BF16, name="xgrp", tag="xgrp", align_bytes=64)
            xgrp[g] = grp
            tr = pool.tile([P, 2, 2, P], F32, name="tr", tag=tag)
            for a in (0, 1):
                turn(words, 512 * a, g, tr[:, a, :, :])
            copy_on(eng, grp[:].bitcast(F32).rearrange("p (a n u) -> p a n u", a=2, u=2), tr[:].rearrange("p a u n -> p a n u"))

        def x_quant(g):
            nc.vector.quantize_mx(out=x_codes[:, g, :].bitcast(FP8X4), scales=x_scales[:, g, :], in_=xgrp[g][:])

        wgrp = {}

        def w_copy(m, g, c0, c1, eng):
            raw = wraw[(m, g, c0 // 512)]
            grp = wst.tile([P, c1 - c0, 4], BF16, name="wgrp", tag="wgrp", align_bytes=64)
            wgrp[(m, g, c0)] = grp
            copy_on(
                eng,
                grp[:].rearrange("p (b m) t -> p b m t", b=2),
                raw[:, :, c0 % 512 : c0 % 512 + c1 - c0].rearrange("p t (m b) -> p b m t", b=2),
            )

        def w_quant(m, g, c0, c1):
            nc.vector.quantize_mx(
                out=w_codes[:, m, g, c0:c1].bitcast(FP8X4),
                scales=w_scales[:, m, g, c0:c1],
                in_=wgrp[(m, g, c0)][:].rearrange("p w t -> p (w t)"),
            )

        xps = {}

        def xf_mm(sc, fill=0):
            ps = ps_tr.tile([P, 2, NODES], F32, name="xps", tag="tr")
            xps[sc] = ps
            for jj in (0, 1):
                cols = slice(P * (2 * sc + jj), P * (2 * sc + jj + 1))
                for g in (0, 1):
                    nc.tensor.matmul_mx(
                        out=ps[:, jj, :],
                        lhsT=w_codes[:, 0, g, cols].bitcast(FP8X4),
                        lhsT_scale=w_scales[:, 0, g, cols],
                        rhs=x_codes[:, g, :].bitcast(FP8X4),
                        rhs_scale=x_scales[:, g, :],
                        start=(g == 0),
                        stop=(g == 1),
                    )
                    if jj == 0 and g == 0:
                        warm_pe(fill)

        def xf_ev(sc):
            for jj in (0, 1):
                j = 2 * sc + jj
                nc.scalar.activation(out=xfT[:, j, :], in_=xps[sc][:, jj, :], func=ACT.Identity, bias=bsum[:, j : j + 1], scale=1.0)

        steps = [(a, q, jp) for a in (0, 1) for q in (0, 1) for jp in (0, 1)]
        steps += [(a, q, jp) for a in (0, 1) for jp in (2, 3) for q in (0, 1)]
        NS = len(steps)
        z_t, ct_t, zz_t, f_t, p_t, o_t, pw_t = {}, {}, {}, {}, {}, {}, {}

        def mx(s, bs=(0, 1)):
            a, q, jp = steps[s]
            qc = slice(512 * q, 512 * (q + 1))
            ac = slice(P * a, P * (a + 1))
            for b in bs:
                z = ps_z.tile([P, 512], F32, name="z", tag="z")
                z_t[(s, b)] = z
                jc = slice(P * (2 * jp + b), P * (2 * jp + b + 1))
                on_pe = (s, b) in XPE
                for g in (0, 1):
                    nc.tensor.matmul_mx(
                        out=z[:],
                        lhsT=w_codes[:, 1, g, jc].bitcast(FP8X4),
                        lhsT_scale=w_scales[:, 1, g, jc],
                        rhs=h_codes[:, a, g, qc].bitcast(FP8X4),
                        rhs_scale=h_scales[:, a, g, qc],
                        start=(g == 0),
                        stop=(g == 1 and not on_pe),
                    )
                if on_pe:
                    for g in (0, 1):
                        for kk in range(4):
                            nc.tensor.matmul_mx(
                                out=z[:, P * kk : P * (kk + 1)],
                                lhsT=w_codes[:, 0, g, jc].bitcast(FP8X4),
                                lhsT_scale=w_scales[:, 0, g, jc],
                                rhs=x_codes[:, g, ac].bitcast(FP8X4),
                                rhs_scale=x_scales[:, g, ac],
                                start=False,
                                stop=(g == 1 and kk == 3),
                            )

        def ct(s):
            a, q, jp = steps[s]
            t = ps_ct.tile([P, 4, P], F32, name="ct", tag="ct")
            ct_t[s] = t
            src = c_sb[(a, q, jp // 2)]
            c0 = 256 * (jp % 2)
            for kk in range(4):
                nc.tensor.transpose(t[:, kk, :], src[:, kk, c0 : c0 + 256].bitcast(F32), ident_f[:])

        def add_x(s, b):
            a, q, jp = steps[s]
            if (s, b) in XPE:
                return
            zz = zzp.tile([P, 512], F32, name="zz", tag="zz")
            zz_t[(s, b)] = zz
            nc.vector.tensor_tensor(
                out=zz[:].rearrange("p (k n) -> p k n", k=4),
                in0=z_t[(s, b)][:].rearrange("p (k n) -> p k n", k=4),
                in1=xfT[:, 2 * jp + b, P * a : P * (a + 1)].unsqueeze(1).to_broadcast([P, 4, P]),
                op=ALU.add,
            )

        def gate(s, b):
            j = 2 * steps[s][2] + b
            if b == 0:
                f_new = fpl.tile([P, 2, 512], F32, name="f", tag="f")
                f_t[s] = f_new
            if (s, b) in XPE:
                nc.scalar.activation(out=f_t[s][:, b, :], in_=z_t[(s, b)][:], func=ACT.Sigmoid, bias=bsum[:, j : j + 1], scale=1.0)
            else:
                nc.scalar.activation(out=f_t[s][:, b, :], in_=zz_t[(s, b)][:], func=ACT.Sigmoid)

        def times_c(s):
            a, q, jp = steps[s]
            p = ppl.tile([P, 2, 512], F32, name="p", tag="p")
            pw_t[(a, q, jp)] = p
            for b in (0, 1):
                p_t[(a, q, jp, b)] = p[:, b, :]
            c_view = ct_t[s][:].rearrange("p k n -> p (k n)").bitcast(BF16).rearrange("p (x e) -> p e x", e=2)
            if s == NS - 1:
                for b in (0, 1):
                    nc.vector.tensor_tensor(out=p[:, b, :], in0=f_t[s][:, b, :], in1=c_view[:, b, :], op=ALU.mult)
            else:
                nc.vector.tensor_tensor(out=p[:], in0=f_t[s][:], in1=c_view, op=ALU.mult)

        cts_t = {}

        def ct_out(s):
            t = ctp.tile([P, 512], F32, name="cts", tag="cts")
            cts_t[s] = t
            nc.scalar.copy(out=t[:], in_=ct_t[s][:].rearrange("p k n -> p (k n)"))

        def times_c_g(s):
            a, q, jp = steps[s]
            p = ppl.tile([P, 2, 512], F32, name="p", tag="p")
            pw_t[(a, q, jp)] = p
            for b in (0, 1):
                p_t[(a, q, jp, b)] = p[:, b, :]
            nc.gpsimd.tensor_tensor(
                out=p[:],
                in0=f_t[s][:],
                in1=cts_t[s][:].bitcast(BF16).rearrange("p (x e) -> p e x", e=2),
                op=ALU.mult,
            )

        def add_up(s, bs=(0, 1)):
            a, q, jp = steps[s]
            if 0 in bs:
                o_new = ps_tr.tile([P, 2, P], F32, name="o", tag="tr")
                o_t[s] = o_new
            o = o_t[s]
            for b in bs:
                srcs = [pa_t[(a, jp, b)]] if (a, jp, b) in pa_t else [p_t[(a, 0, jp, b)], p_t[(a, 1, jp, b)]]
                for n, src in enumerate(srcs):
                    for kk in range(4):
                        nc.tensor.matmul(
                            out=o[:, b, :],
                            lhsT=src[:, P * kk : P * (kk + 1)],
                            rhs=ident_f[:],
                            is_transpose=True,
                            start=(n == 0 and kk == 0),
                            stop=(n == len(srcs) - 1 and kk == 3),
                        )

        pa_t = {}

        def pre_add(s):
            a, q, jp = steps[s]
            t = pap.tile([P, 2, 512], F32, name="pa", tag="pa")
            for b in (0, 1):
                pa_t[(a, jp, b)] = t[:, b, :]
            nc.gpsimd.tensor_tensor(out=t[:], in0=pw_t[(a, 0, jp)][:], in1=pw_t[(a, 1, jp)][:], op=ALU.add)

        n_done = [0]
        pmax = keep.tile([P, 1], F32, name="pmax")

        def leave(s):
            a, q, jp = steps[s]
            cols = slice(256 * jp, 256 * (jp + 1))
            here = slice(H * a + 256 * jp, H * a + 256 * (jp + 1))
            nc.scalar.copy(out=out_sb[:, here].rearrange("p (m b) -> p m b", b=2), in_=o_t[s][:].rearrange("p b m -> p m b"))
            nc.sync.dma_start(out=out_0[P * a : P * (a + 1), cols], in_=out_sb[:, here])

        def peak(s):
            a, q, jp = steps[s]
            c0 = H * a + 256 * jp
            i = n_done[0]
            n_done[0] = i + 1
            if i < 7:
                nc.vector.tensor_reduce(
                    out=out_sb[:, 2 * H + i : 2 * H + i + 1], in_=out_sb[:, c0 : c0 + 256], axis=AX.X, op=ALU.max, apply_absolute_value=True
                )
            else:
                assert c0 + 256 == 2 * H
                nc.vector.tensor_reduce(out=pmax[:], in_=out_sb[:, c0 : 2 * H + 7], axis=AX.X, op=ALU.max, apply_absolute_value=True)

        warm_pe(6)
        for i in (0, 1):
            h_tr(0, 0, 0, i)
            h_cp(0, 0, 0, i, "s")
            h_tr(0, 0, 1, i, ps_z, "z")
            h_cp(0, 0, 1, i, "s")
        h_quant(0, 0, 0)
        x_turn(0, "s")
        x_turn(1, "s", ps_z, "z")
        warm_pe(0)
        h_quant(0, 0, 1)
        w_copy(0, 0, 0, 256, "v")
        w_copy(0, 0, 256, 512, "s")
        x_quant(0)
        w_quant(0, 0, 0, 256)
        x_quant(1)
        w_copy(0, 1, 0, 256, "v")
        w_copy(0, 1, 256, 512, "s")
        w_quant(0, 0, 256, 512)
        w_quant(0, 1, 0, 256)
        bias()
        xf_mm(0, 0)
        w_copy(1, 0, 0, 256, "v")
        w_copy(1, 0, 256, 512, "s")
        w_quant(0, 1, 256, 512)
        xf_mm(1, 0)
        w_quant(1, 0, 0, 256)
        xf_ev(0)
        w_copy(1, 1, 0, 256, "v")
        w_copy(1, 1, 256, 512, "s")
        w_quant(1, 0, 256, 512)
        w_quant(1, 1, 0, 256)
        h_tr(0, 1, 0, 0, ps_ct, "ct")
        h_cp(0, 1, 0, 0, "s")
        h_tr(0, 1, 1, 0)
        h_cp(0, 1, 1, 0, "s")
        mx(0)
        xf_ev(1)
        w_quant(1, 1, 256, 512)
        h_quant_half(0, 1, 0, 0)
        h_quant_half(0, 1, 1, 0)
        h_tr(0, 1, 0, 1, ps_ct, "ct")
        h_cp(0, 1, 0, 1, "s")
        h_tr(0, 1, 1, 1)
        h_cp(0, 1, 1, 1, "s")

        HT = {0: (1, 0, 0), 1: (1, 0, 1), 2: (1, 1, 0), 3: (1, 1, 1)}
        CP = {4: (0, 512), 5: (1, 512), 6: (0, 768), 7: (1, 768)}
        QU = {5: (0, 512), 6: (1, 512), 7: (0, 768), 8: (1, 768)}
        QM = {}
        XF = {5: 2, 7: 3}

        def t_extra(s):
            if s in HT:
                a, q, g = HT[s]
                for i in (0, 1):
                    h_tr(a, q, g, i)
                    h_cp(a, q, g, i, "s")
            if s in XF:
                xf_mm(XF[s])
                xf_ev(XF[s])

        def s_extra(s):
            if s in CP:
                m, c0 = CP[s]
                w_copy(m, 0, c0, c0 + 256, "s")
                w_copy(m, 1, c0, c0 + 256, "g")

        def v_extra(s):
            if s == 0:
                h_quant_half(0, 1, 0, 1)
                h_quant_half(0, 1, 1, 1)
            if s - 1 in HT:
                a, q, g = HT[s - 1]
                h_quant(a, q, g)
            if s in QU:
                m, c0 = QU[s]
                w_quant(m, 0, c0, c0 + 256)
                w_quant(m, 1, c0, c0 + 256)

        def is_last_q(s):
            return 0 <= s < NS and steps[s][1] == 1

        todo = []
        left = []
        seen = []
        for s in range(NS + 4):
            late = s in QM
            if s + 1 < NS and not late:
                mx(s + 1, (0,))
            if left:
                leave(left[0])
                seen.append(left[0])
                left.remove(left[0])
            if s < NS:
                add_x(s, 0)
                gate(s, 0)
            if s + 1 < NS and not late:
                mx(s + 1, (1,))
            if s < NS:
                add_x(s, 1)
                gate(s, 1)
                ct(s)
                if s in GS:
                    ct_out(s)
                    times_c_g(s)
            s_extra(s)
            for n in range(1 if s < NS else 2):
                if todo:
                    add_up(todo[0][0], (todo[0][1],))
                    if todo[0][1] == 1:
                        left.append(todo[0][0])
                    todo.remove(todo[0])
            if late:
                m, c0 = QM[s]
                w_quant(m, 0, c0, c0 + 256)
                w_quant(m, 1, c0, c0 + 256)
                mx(s + 1)
            if 1 <= s <= NS:
                if s - 1 not in GS:
                    times_c(s - 1)
                if is_last_q(s - 1):
                    if s - 1 in PS:
                        pre_add(s - 1)
                    todo.extend([(s - 1, 0), (s - 1, 1)])
            v_extra(s)
            t_extra(s)
            if seen and (s >= NS or len(seen) > 1 or not left):
                peak(seen[0])
                seen.remove(seen[0])

        aps = ps_tr.tile([P, P], F32, name="aps", tag="tr")
        nc.tensor.transpose(aps[:], pmax[:, 0:1].to_broadcast([P, P]), ident_f[:])
        scaled = keep.tile([P, P], F32, name="scaled")
        scl = keep.tile([P, 1], F32, name="scl")
        nc.vector.tensor_scalar(out=scaled[:], in0=aps[:], scalar1=1.0 / 448.0, scalar2=None, op0=ALU.mult, op1=ALU.max, accum_out=scl[:])
        fac = keep.tile([P, 1], F32, name="fac")
        nc.vector.reciprocal(out=fac[:], in_=scl[:])

        o8a = keep.tile([P, H], FP8, name="o8a")
        o8b = keep.tile([P, H], FP8, name="o8b")
        VS = 384
        nc.scalar.activation(
            out=o8b[:, VS:H], in_=out_sb[:, H + VS : 2 * H], func=ACT.Identity, scale=fac[:, 0:1], bias=zero_col[:, 0:1], saturate=False
        )
        nc.vector.tensor_scalar(out=o8a[:], in0=out_sb[:, 0:H], scalar1=fac[:, 0:1], scalar2=None, op0=ALU.mult, saturate=False)
        nc.sync.dma_start(out=out_1[0:P, :], in_=o8a[:].bitcast(U8))
        nc.vector.tensor_scalar(
            out=o8b[:, 0:VS], in0=out_sb[:, H : H + VS], scalar1=fac[:, 0:1], scalar2=None, op0=ALU.mult, saturate=False
        )
        nc.sync.dma_start(out=out_1[P : 2 * P, :], in_=o8b[:].bitcast(U8))
